import numpy as np
import ml_dtypes


def mxq(x, axis, fmt="e4m3"):
    dtype, down = {"e4m3": (ml_dtypes.float8_e4m3fn, 7), "e5m2": (ml_dtypes.float8_e5m2, 14)}[fmt]
    v = np.moveaxis(np.asarray(x, np.float32).astype(ml_dtypes.bfloat16).astype(np.float64), axis, -1)
    blocks = v.reshape(v.shape[:-1] + (-1, 32))
    amax = np.abs(blocks).max(-1, keepdims=True)
    byte = np.maximum(np.where(amax > 0, np.frexp(amax)[1] - 1 + 127, 0) - down, 1)
    scale = np.exp2(byte - 127.0)
    codes = (blocks / scale).astype(np.float32).astype(dtype).astype(np.float64)
    return np.moveaxis((codes * scale).reshape(v.shape), -1, axis)


WIDE = False


def mx_kscale(k):
    if not WIDE:
        return np.ones(k)
    levels = np.array([20, -20, 10, -10, 0])
    a = np.random.permutation(np.resize(levels, k // 512 * 4)).reshape(k // 512, 4)
    idx = np.arange(k)
    return np.exp2(a[idx // 512, idx % 128 // 32])


BF16 = ml_dtypes.bfloat16


def bf(x):
    return np.asarray(x, np.float32).astype(BF16)


def f64(x):
    return np.asarray(x).astype(np.float64)


B, I, H = 512, 512, 1024


def sigmoid(v):
    return 1.0 / (1.0 + np.exp(-v))


def setup_inputs():
    u = mx_kscale(H)
    u4 = np.tile(u, 4)
    t = bf(np.random.uniform(0.5, 2.0, (B, 1)) * (np.random.random((B, 1)) >= 0.125))
    x = bf(np.random.standard_normal((B, I)))
    hx = bf(np.random.standard_normal((B, H)))
    cx = bf(np.random.standard_normal((B, H)))
    wih0 = bf(np.random.standard_normal((4 * H, I)) * 0.8 / np.sqrt(I))
    whh = bf(np.random.standard_normal((4 * H, H)) * 0.8 / np.sqrt(H))
    bih = bf(np.random.standard_normal(4 * H) * 0.4)
    bhh = bf(np.random.standard_normal(4 * H) * 0.4)
    wd = bf(np.random.standard_normal((H, H)) / np.sqrt(H))
    bd = bf(np.random.standard_normal(H) * 0.5)
    g = bf(np.random.standard_normal((2, B, H)) * np.exp2(np.random.randint(-12, 1, (1, B, 1))) * 32.0 * u[None, None, :])
    gates = f64(x) @ f64(wih0).T + f64(bih) + f64(hx) @ f64(whh).T + f64(bhh)
    tf = f64(t)
    T = np.where(tf != 0, 1.0 / np.where(tf != 0, tf, 1.0), 0.0)
    C_ST = np.tanh(f64(cx) @ f64(wd) + f64(bd))
    cx_adj = f64(cx) - C_ST + T * C_ST
    return {"input": x, "t": t, "hx": hx, "cx": cx,
            "weight_ih": bf(f64(wih0) / u4[:, None]),
            "weight_hh": whh, "bias_ih": bih, "bias_hh": bhh,
            "W_decomp": wd, "b_decomp": bd,
            "gates": np.asarray(gates, np.float32),
            "cx_adj": np.asarray(cx_adj, np.float32),
            "grad_out": g}


def reference(input, t, hx, cx, weight_ih, weight_hh, bias_ih, bias_hh, W_decomp, b_decomp, gates, cx_adj, grad_out):
    zi, zf, zg, zo = np.split(f64(gates), 4, axis=1)
    ca = f64(cx_adj)
    go = f64(grad_out)
    g_hy, g_cy = go[0], go[1]
    i = sigmoid(zi)
    f = sigmoid(zf)
    g = np.tanh(zg)
    o = sigmoid(zo)
    tc = np.tanh(f * ca + i * g)
    d_cy = g_cy + g_hy * (o * (1.0 - tc * tc))
    d_i = d_cy * (g * i * (1.0 - i))
    d_f = d_cy * (ca * f * (1.0 - f))
    d_g = d_cy * (i * (1.0 - g * g))
    d_o = g_hy * (tc * o * (1.0 - o))
    dgates = np.concatenate([d_i, d_f, d_g, d_o], axis=1)
    return mxq(dgates, 1, "e5m2") @ mxq(f64(weight_ih), 0, "e4m3")

@@ -1,0 +1,249 @@
+import math
+from contextlib import ExitStack
+
+import concourse.mybir as mybir
+from concourse.masks import make_identity
+
+F32 = mybir.dt.float32
+BF16 = mybir.dt.bfloat16
+U32 = mybir.dt.uint32
+U8 = mybir.dt.uint8
+E4M3_X4 = mybir.dt.float8_e4m3fn_x4
+E5M2_X4 = mybir.dt.float8_e5m2_x4
+ADD = mybir.AluOpType.add
+SUB = mybir.AluOpType.subtract
+MULT = mybir.AluOpType.mult
+TANH = mybir.ActivationFunctionType.Tanh
+SQUARE = mybir.ActivationFunctionType.Square
+
+B, I_DIM, H = 512, 512, 1024
+P = 128
+PACK = 4
+K_PASS = P * PACK
+GATES = 4
+GATE_I, GATE_F, GATE_G, GATE_O = 0, 1, 2, 3
+HALVES = H // K_PASS
+GROUPS = (B // P) * HALVES
+
+FLOPS = 2 * B * GATES * H * I_DIM
+BYTES = 4 * B * GATES * H + 4 * B * H + 2 * 2 * B * H + 2 * GATES * H * I_DIM + 4 * B * I_DIM
+
+
+def tile_ta_lstmcell_v_kernel(
+    tc, x_in, t_in, hx, cx, weight_ih, weight_hh, bias_ih, bias_hh, w_decomp, b_decomp,
+    gates, cx_adj, grad_out, out,
+):
+    nc = tc.nc
+    tiles = {}
+
+    with ExitStack() as stack:
+        const = stack.enter_context(tc.tile_pool(name="const", bufs=1))
+        raw = stack.enter_context(tc.tile_pool(name="raw", bufs=3))
+        acts = stack.enter_context(tc.tile_pool(name="acts", bufs=3))
+        work = stack.enter_context(tc.tile_pool(name="work", bufs=2))
+        codes = stack.enter_context(tc.tile_pool(name="codes", bufs=GROUPS))
+        psum = stack.enter_context(tc.psum_pool(name="psum", bufs=1))
+        stack.enter_context(tc.manual_schedule())
+
+        ident_f32 = const.tile([P, P], F32)
+        make_identity(nc, ident_f32[:])
+        ident_bf16 = const.tile([P, P], BF16)
+        make_identity(nc, ident_bf16[:])
+        w_codes = const.tile([P, GATES * HALVES, I_DIM], U32, align_bytes=64)
+        w_scales = const.tile([P, GATES * HALVES, I_DIM], U8, align_bytes=64)
+
+        def batch_rows(n):
+            return slice((n // HALVES) * P, (n // HALVES + 1) * P)
+
+        def hidden_cols(n, start=0):
+            return slice(start + (n % HALVES) * K_PASS, start + (n % HALVES + 1) * K_PASS)
+
+        def new(pool, name, n, dtype=F32, shape=(P, K_PASS), **kw):
+            tiles[(name, n)] = pool.tile(list(shape), dtype, name=name, tag=name, **kw)
+            return tiles[(name, n)]
+
+        def got(name, n):
+            return tiles[(name, n)]
+
+        def by_batch(flat):
+            return flat.rearrange("p (b t) -> p b t", t=PACK)
+
+        def bank_by_batch(bank):
+            return bank.rearrange("p t b -> p b t")
+
+        def load_group(n):
+            for q in (GATE_F, GATE_I, GATE_G, GATE_O):
+                z_raw = new(raw, "z_raw%d" % q, n)
+                nc.sync.dma_start(out=z_raw[:], in_=gates[batch_rows(n), hidden_cols(n, q * H)])
+                if q == GATE_F:
+                    ca_raw = new(raw, "ca_raw", n)
+                    nc.sync.dma_start(out=ca_raw[:], in_=cx_adj[batch_rows(n), hidden_cols(n)])
+            g_raw = new(raw, "g_raw", n, BF16, (P, 2, K_PASS))
+            nc.sync.dma_start(
+                out=g_raw[:],
+                in_=grad_out[:, batch_rows(n), hidden_cols(n)].rearrange("s b h -> b s h"),
+            )
+
+        def load_weight(q):
+            w_raw = new(const, "w_raw%d" % q, q, BF16, (P, HALVES, PACK, I_DIM))
+            nc.sync.dma_start(
+                out=w_raw[:],
+                in_=weight_ih[q * H : (q + 1) * H, :].rearrange("(c t p) n -> p c t n", t=PACK, p=P),
+            )
+
+        def transpose_into(bank, src, ident):
+            for t in range(PACK):
+                nc.tensor.transpose(bank[:, t, :], src[:, t * P : (t + 1) * P], ident[:])
+
+        def gate_tanhs(n):
+            for q in (GATE_F, GATE_I, GATE_G, GATE_O):
+                z_bank = psum.tile([P, PACK, P], F32, tag="z", bufs=3)
+                transpose_into(z_bank, got("z_raw%d" % q, n), ident_f32)
+                th = new(acts, "tanh%d" % q, n)
+                nc.scalar.activation(
+                    out=by_batch(th[:]), in_=bank_by_batch(z_bank[:]), func=TANH,
+                    scale=1.0 if q == GATE_G else 0.5,
+                )
+            half_g2 = new(acts, "half_g2", n)
+            nc.scalar.activation(out=half_g2[:], in_=got("tanh%d" % GATE_G, n)[:], func=SQUARE, scale=math.sqrt(0.5))
+
+        def transpose_ca(n):
+            transpose_into(new(psum, "ca", n, F32, (P, PACK, P)), got("ca_raw", n), ident_f32)
+
+        def transpose_ghy(n):
+            transpose_into(new(psum, "ghy", n, BF16, (P, PACK, P)), got("g_raw", n)[:, 0, :], ident_bf16)
+
+        def transpose_gcy(n):
+            transpose_into(new(psum, "gcy", n, BF16, (P, PACK, P)), got("g_raw", n)[:, 1, :], ident_bf16)
+
+        def stt(out, in0, scalar, in1, op0, op1):
+            nc.vector.scalar_tensor_tensor(out=out, in0=in0, scalar=scalar, in1=in1, op0=op0, op1=op1)
+
+        def op_m1(n):
+            stt(by_batch(new(work, "m1", n)[:]), by_batch(got("tanh%d" % GATE_F, n)[:]), 1.0,
+                bank_by_batch(got("ca", n)[:]), ADD, MULT)
+
+        def op_m2(n):
+            stt(new(work, "m2", n)[:], got("tanh%d" % GATE_I, n)[:], 1.0, got("tanh%d" % GATE_G, n)[:], ADD, MULT)
+
+        def op_s(n):
+            nc.vector.tensor_tensor(out=new(work, "s", n)[:], in0=got("m1", n)[:], in1=got("m2", n)[:], op=ADD)
+
+        def act_tc(n):
+            nc.scalar.activation(out=new(work, "tc", n)[:], in_=got("s", n)[:], func=TANH, scale=0.5)
+            nc.scalar.activation(out=new(work, "tc2", n)[:], in_=got("tc", n)[:], func=SQUARE)
+
+        def op_ho(n):
+            stt(by_batch(new(work, "ho", n)[:]), by_batch(got("tanh%d" % GATE_O, n)[:]), 1.0,
+                bank_by_batch(got("ghy", n)[:]), ADD, MULT)
+
+        def op_q(n):
+            stt(new(work, "q", n)[:], got("tanh%d" % GATE_O, n)[:], -1.0, got("ho", n)[:], ADD, MULT)
+
+        def op_pi(n):
+            stt(new(work, "pi", n)[:], got("tanh%d" % GATE_I, n)[:], -1.0, got("m2", n)[:], ADD, MULT)
+
+        def op_pf(n):
+            stt(new(work, "pf", n)[:], got("tanh%d" % GATE_F, n)[:], -1.0, got("m1", n)[:], ADD, MULT)
+
+        def op_d_o(n):
+            dq = new(work, "dq", n, BF16, (P, GATES, K_PASS), align_bytes=64)
+            stt(dq[:, GATE_O, :], got("q", n)[:], -0.25, got("tc", n)[:], MULT, MULT)
+
+        def op_e(n):
+            stt(new(work, "e", n)[:], got("tc2", n)[:], -1.0, got("ho", n)[:], ADD, MULT)
+
+        def op_dn(n):
+            stt(by_batch(new(work, "dn", n)[:]), by_batch(got("e", n)[:]), 0.5,
+                bank_by_batch(got("gcy", n)[:]), MULT, SUB)
+
+        def op_d_i(n):
+            stt(got("dq", n)[:, GATE_I, :], got("pi", n)[:], 0.25, got("dn", n)[:], MULT, MULT)
+
+        def op_d_f(n):
+            stt(got("dq", n)[:, GATE_F, :], got("pf", n)[:], 0.25, got("dn", n)[:], MULT, MULT)
+
+        def op_eg(n):
+            stt(new(work, "eg", n)[:], got("half_g2", n)[:], -0.5, got("dn", n)[:], ADD, MULT)
+
+        def op_d_g(n):
+            stt(got("dq", n)[:, GATE_G, :], got("tanh%d" % GATE_I, n)[:], 1.0, got("eg", n)[:], ADD, MULT)
+
+        def quantise_dgates(n):
+            nc.vector.quantize_mx(
+                out=new(codes, "d_codes", n, U32, (P, GATES * P), align_bytes=64)[:].bitcast(E5M2_X4),
+                scales=new(codes, "d_scales", n, U8, (P, GATES * P), align_bytes=64)[:],
+                in_=got("dq", n)[:].rearrange("p q c -> p (q c)"),
+            )
+
+        def regroup_weight(q, c):
+            if c == 0:
+                new(work, "w_grouped", q, BF16, (P, HALVES, I_DIM, PACK), align_bytes=64)
+            nc.scalar.copy(
+                out=got("w_grouped", q)[:, c].rearrange("p (m i) t -> p m t i", i=4),
+                in_=got("w_raw%d" % q, q)[:, c].rearrange("p t (m i) -> p m t i", i=4),
+            )
+
+        def quantise_weight(q):
+            passes = slice(q * HALVES, (q + 1) * HALVES)
+            nc.vector.quantize_mx(
+                out=w_codes[:, passes, :].rearrange("p c n -> p (c n)").bitcast(E4M3_X4),
+                scales=w_scales[:, passes, :].rearrange("p c n -> p (c n)"),
+                in_=got("w_grouped", q)[:].rearrange("p c n t -> p (c n t)"),
+            )
+
+        def multiply(n):
+            b_tile, half = divmod(n, HALVES)
+            if half == 0:
+                new(psum, "acc", b_tile, F32, (P, I_DIM), bufs=2)
+            acc = got("acc", b_tile)
+            for q in range(GATES):
+                nc.tensor.matmul_mx(
+                    out=acc[:],
+                    lhsT=got("d_codes", n)[:, q * P : (q + 1) * P].bitcast(E5M2_X4),
+                    lhsT_scale=got("d_scales", n)[:, q * P : (q + 1) * P],
+                    rhs=w_codes[:, q * HALVES + half, :].bitcast(E4M3_X4),
+                    rhs_scale=w_scales[:, q * HALVES + half, :],
+                    start=(half == 0 and q == 0),
+                    stop=(half == HALVES - 1 and q == GATES - 1),
+                )
+            if half == HALVES - 1:
+                result = work.tile([P, I_DIM], F32)
+                nc.scalar.copy(out=result[:], in_=acc[:])
+                nc.sync.dma_start(out=out[batch_rows(n), :], in_=result[:])
+
+        def run(step, n, count=GROUPS):
+            if 0 <= n < count:
+                step(n)
+
+        for j in range(-3, GROUPS):
+            run(load_group, j + 3)
+            run(load_weight, j + 2, GATES)
+            if 0 <= j < GATES:
+                regroup_weight(j, 0)
+            run(op_m1, j + 1)
+            run(op_d_o, j)
+            run(op_m2, j + 1)
+            run(op_e, j)
+            run(op_s, j + 1)
+            run(act_tc, j + 1)
+            run(op_dn, j)
+            run(op_ho, j + 1)
+            run(op_d_i, j)
+            run(op_q, j + 1)
+            run(op_d_f, j)
+            run(op_pi, j + 1)
+            run(op_eg, j)
+            run(op_pf, j + 1)
+            run(op_d_g, j)
+            run(gate_tanhs, j + 2)
+            run(transpose_ca, j + 2)
+            run(transpose_ghy, j + 2)
+            run(transpose_gcy, j + 1)
+            if 0 <= j < GATES:
+                regroup_weight(j, 1)
+            run(quantise_weight, j - 1, GATES)
+            run(quantise_dgates, j)
+            if j >= GATES:
+                for n in range(0 if j == GATES else j, j + 1):
+                    multiply(n)

@@ -11,7 +11,6 @@ U8 = mybir.dt.uint8
 E4M3_X4 = mybir.dt.float8_e4m3fn_x4
 E5M2_X4 = mybir.dt.float8_e5m2_x4
 ADD = mybir.AluOpType.add
-SUB = mybir.AluOpType.subtract
 MULT = mybir.AluOpType.mult
 TANH = mybir.ActivationFunctionType.Tanh
 SQUARE = mybir.ActivationFunctionType.Square
@@ -24,6 +23,8 @@ GATES = 4
 GATE_I, GATE_F, GATE_G, GATE_O = 0, 1, 2, 3
 HALVES = H // K_PASS
 GROUPS = (B // P) * HALVES
+W_PIECES = 4
+W_PIECE_COLS = HALVES * I_DIM // W_PIECES
 
 FLOPS = 2 * B * GATES * H * I_DIM
 BYTES = 4 * B * GATES * H + 4 * B * H + 2 * 2 * B * H + 2 * GATES * H * I_DIM + 4 * B * I_DIM
@@ -47,8 +48,6 @@ def tile_ta_lstmcell_v_kernel(
 
         ident_f32 = const.tile([P, P], F32)
         make_identity(nc, ident_f32[:])
-        ident_bf16 = const.tile([P, P], BF16)
-        make_identity(nc, ident_bf16[:])
         w_codes = const.tile([P, GATES * HALVES, I_DIM], U32, align_bytes=64)
         w_scales = const.tile([P, GATES * HALVES, I_DIM], U8, align_bytes=64)
 
@@ -65,109 +64,98 @@ def tile_ta_lstmcell_v_kernel(
         def got(name, n):
             return tiles[(name, n)]
 
-        def by_batch(flat):
+        def packed(flat):
             return flat.rearrange("p (b t) -> p b t", t=PACK)
 
-        def bank_by_batch(bank):
-            return bank.rearrange("p t b -> p b t")
+        def turned(flat):
+            return flat.rearrange("p (t b) -> p b t", t=PACK)
 
         def load_group(n):
-            for q in (GATE_F, GATE_I, GATE_G, GATE_O):
-                z_raw = new(raw, "z_raw%d" % q, n)
-                nc.sync.dma_start(out=z_raw[:], in_=gates[batch_rows(n), hidden_cols(n, q * H)])
-                if q == GATE_F:
-                    ca_raw = new(raw, "ca_raw", n)
-                    nc.sync.dma_start(out=ca_raw[:], in_=cx_adj[batch_rows(n), hidden_cols(n)])
-            g_raw = new(raw, "g_raw", n, BF16, (P, 2, K_PASS))
+            for name, start in (("zf", GATE_F * H), ("ca", None), ("zi", GATE_I * H), ("zg", GATE_G * H), ("zo", GATE_O * H)):
+                src = cx_adj[batch_rows(n), hidden_cols(n)] if start is None else gates[batch_rows(n), hidden_cols(n, start)]
+                nc.sync.dma_start(out=new(raw, name, n)[:], in_=src)
             nc.sync.dma_start(
-                out=g_raw[:],
+                out=new(raw, "grads", n, BF16, (P, 2, K_PASS))[:],
                 in_=grad_out[:, batch_rows(n), hidden_cols(n)].rearrange("s b h -> b s h"),
             )
 
         def load_weight(q):
-            w_raw = new(const, "w_raw%d" % q, q, BF16, (P, HALVES, PACK, I_DIM))
             nc.sync.dma_start(
-                out=w_raw[:],
+                out=new(const, "w_raw%d" % q, q, BF16, (P, HALVES, PACK, I_DIM))[:],
                 in_=weight_ih[q * H : (q + 1) * H, :].rearrange("(c t p) n -> p c t n", t=PACK, p=P),
             )
 
-        def transpose_into(bank, src, ident):
+        def turn(name, n, terms, **kw):
+            bank = new(psum, name, n, **kw)
             for t in range(PACK):
-                nc.tensor.transpose(bank[:, t, :], src[:, t * P : (t + 1) * P], ident[:])
+                block = slice(t * P, (t + 1) * P)
+                for term in terms:
+                    nc.tensor.matmul(
+                        out=bank[:, block], lhsT=term[:, block], rhs=ident_f32[:], is_transpose=True,
+                        start=(term is terms[0]), stop=(term is terms[-1]),
+                    )
+            return bank
 
-        def gate_tanhs(n):
-            for q in (GATE_F, GATE_I, GATE_G, GATE_O):
-                z_bank = psum.tile([P, PACK, P], F32, tag="z", bufs=3)
-                transpose_into(z_bank, got("z_raw%d" % q, n), ident_f32)
-                th = new(acts, "tanh%d" % q, n)
-                nc.scalar.activation(
-                    out=by_batch(th[:]), in_=bank_by_batch(z_bank[:]), func=TANH,
-                    scale=1.0 if q == GATE_G else 0.5,
-                )
-            half_g2 = new(acts, "half_g2", n)
-            nc.scalar.activation(out=half_g2[:], in_=got("tanh%d" % GATE_G, n)[:], func=SQUARE, scale=math.sqrt(0.5))
+        def act(name, n, pool, src, func, scale=1.0):
+            nc.scalar.activation(out=new(pool, name, n)[:], in_=src[:], func=func, scale=scale)
 
-        def transpose_ca(n):
-            transpose_into(new(psum, "ca", n, F32, (P, PACK, P)), got("ca_raw", n), ident_f32)
+        def first_acts(n):
+            act("tf", n, acts, turn("z", n, [got("zf", n)], bufs=2), TANH, 0.5)
+            turn("ca_t", n, [got("ca", n)])
+            act("ti", n, acts, turn("z", n, [got("zi", n)], bufs=2), TANH, 0.5)
+            act("g", n, acts, turn("z", n, [got("zg", n)], bufs=2), TANH)
+            act("half_g2", n, acts, got("g", n), SQUARE, math.sqrt(0.5))
+            act("to", n, acts, got("zo", n), TANH, 0.5)
+            nc.scalar.mul(out=new(acts, "neg_gcy", n)[:], in_=got("grads", n)[:, 1, :], mul=-1.0)
 
-        def transpose_ghy(n):
-            transpose_into(new(psum, "ghy", n, BF16, (P, PACK, P)), got("g_raw", n)[:, 0, :], ident_bf16)
+        def cell_acts(n):
+            act("tc", n, work, turn("s", n, [got("m1", n), got("m2", n)]), TANH, 0.5)
+            act("half_tc2", n, work, got("tc", n), SQUARE, math.sqrt(0.5))
 
-        def transpose_gcy(n):
-            transpose_into(new(psum, "gcy", n, BF16, (P, PACK, P)), got("g_raw", n)[:, 1, :], ident_bf16)
-
-        def stt(out, in0, scalar, in1, op0, op1):
-            nc.vector.scalar_tensor_tensor(out=out, in0=in0, scalar=scalar, in1=in1, op0=op0, op1=op1)
+        def stt(out, in0, scalar, in1, op0):
+            nc.vector.scalar_tensor_tensor(out=out, in0=in0, scalar=scalar, in1=in1, op0=op0, op1=MULT)
 
         def op_m1(n):
-            stt(by_batch(new(work, "m1", n)[:]), by_batch(got("tanh%d" % GATE_F, n)[:]), 1.0,
-                bank_by_batch(got("ca", n)[:]), ADD, MULT)
+            stt(new(work, "m1", n)[:], got("tf", n)[:], 1.0, got("ca_t", n)[:], ADD)
 
         def op_m2(n):
-            stt(new(work, "m2", n)[:], got("tanh%d" % GATE_I, n)[:], 1.0, got("tanh%d" % GATE_G, n)[:], ADD, MULT)
-
-        def op_s(n):
-            nc.vector.tensor_tensor(out=new(work, "s", n)[:], in0=got("m1", n)[:], in1=got("m2", n)[:], op=ADD)
-
-        def act_tc(n):
-            nc.scalar.activation(out=new(work, "tc", n)[:], in_=got("s", n)[:], func=TANH, scale=0.5)
-            nc.scalar.activation(out=new(work, "tc2", n)[:], in_=got("tc", n)[:], func=SQUARE)
-
-        def op_ho(n):
-            stt(by_batch(new(work, "ho", n)[:]), by_batch(got("tanh%d" % GATE_O, n)[:]), 1.0,
-                bank_by_batch(got("ghy", n)[:]), ADD, MULT)
-
-        def op_q(n):
-            stt(new(work, "q", n)[:], got("tanh%d" % GATE_O, n)[:], -1.0, got("ho", n)[:], ADD, MULT)
-
-        def op_pi(n):
-            stt(new(work, "pi", n)[:], got("tanh%d" % GATE_I, n)[:], -1.0, got("m2", n)[:], ADD, MULT)
+            stt(new(work, "m2", n)[:], got("ti", n)[:], 1.0, got("g", n)[:], ADD)
 
         def op_pf(n):
-            stt(new(work, "pf", n)[:], got("tanh%d" % GATE_F, n)[:], -1.0, got("m1", n)[:], ADD, MULT)
+            stt(new(work, "pf", n)[:], got("tf", n)[:], -1.0, got("m1", n)[:], ADD)
+
+        def op_pi(n):
+            stt(new(work, "pi", n)[:], got("ti", n)[:], -1.0, got("m2", n)[:], ADD)
+
+        def op_ho(n):
+            stt(new(work, "ho", n)[:], got("to", n)[:], 1.0, got("grads", n)[:, 0, :], ADD)
+
+        def op_q(n):
+            stt(new(work, "q", n)[:], got("to", n)[:], -1.0, got("ho", n)[:], ADD)
+
+        def op_xn(n):
+            stt(new(work, "xn", n)[:], got("half_tc2", n)[:], -0.5, got("ho", n)[:], ADD)
 
         def op_d_o(n):
+            stt(new(work, "d_o", n)[:], got("q", n)[:], -0.25, got("tc", n)[:], MULT)
+
+        def turn_cell_grads(n):
+            turn("dn", n, [got("xn", n), got("neg_gcy", n)])
+            d_o_t = turn("d_o_t", n, [got("d_o", n)])
             dq = new(work, "dq", n, BF16, (P, GATES, K_PASS), align_bytes=64)
-            stt(dq[:, GATE_O, :], got("q", n)[:], -0.25, got("tc", n)[:], MULT, MULT)
-
-        def op_e(n):
-            stt(new(work, "e", n)[:], got("tc2", n)[:], -1.0, got("ho", n)[:], ADD, MULT)
-
-        def op_dn(n):
-            stt(by_batch(new(work, "dn", n)[:]), by_batch(got("e", n)[:]), 0.5,
-                bank_by_batch(got("gcy", n)[:]), MULT, SUB)
-
-        def op_d_i(n):
-            stt(got("dq", n)[:, GATE_I, :], got("pi", n)[:], 0.25, got("dn", n)[:], MULT, MULT)
-
-        def op_d_f(n):
-            stt(got("dq", n)[:, GATE_F, :], got("pf", n)[:], 0.25, got("dn", n)[:], MULT, MULT)
+            nc.scalar.copy(out=packed(dq[:, GATE_O, :]), in_=turned(d_o_t[:]))
 
         def op_eg(n):
-            stt(new(work, "eg", n)[:], got("half_g2", n)[:], -0.5, got("dn", n)[:], ADD, MULT)
+            stt(packed(new(work, "eg", n)[:]), turned(got("half_g2", n)[:]), -0.5, turned(got("dn", n)[:]), ADD)
+
+        def op_d_i(n):
+            stt(packed(got("dq", n)[:, GATE_I, :]), turned(got("pi", n)[:]), 0.25, turned(got("dn", n)[:]), MULT)
+
+        def op_d_f(n):
+            stt(packed(got("dq", n)[:, GATE_F, :]), turned(got("pf", n)[:]), 0.25, turned(got("dn", n)[:]), MULT)
 
         def op_d_g(n):
-            stt(got("dq", n)[:, GATE_G, :], got("tanh%d" % GATE_I, n)[:], 1.0, got("eg", n)[:], ADD, MULT)
+            stt(packed(got("dq", n)[:, GATE_G, :]), turned(got("ti", n)[:]), 1.0, packed(got("eg", n)[:]), ADD)
 
         def quantise_dgates(n):
             nc.vector.quantize_mx(
@@ -176,12 +164,14 @@ def tile_ta_lstmcell_v_kernel(
                 in_=got("dq", n)[:].rearrange("p q c -> p (q c)"),
             )
 
-        def regroup_weight(q, c):
-            if c == 0:
-                new(work, "w_grouped", q, BF16, (P, HALVES, I_DIM, PACK), align_bytes=64)
-            nc.scalar.copy(
-                out=got("w_grouped", q)[:, c].rearrange("p (m i) t -> p m t i", i=4),
-                in_=got("w_raw%d" % q, q)[:, c].rearrange("p t (m i) -> p m t i", i=4),
+        def regroup_weight(copy, q, piece):
+            if piece == 0:
+                new(work, "w_grouped", q, BF16, (P, HALVES * I_DIM, PACK), align_bytes=64)
+            c, part = divmod(piece * W_PIECE_COLS, I_DIM)
+            copy(
+                out=got("w_grouped", q)[:, piece * W_PIECE_COLS : (piece + 1) * W_PIECE_COLS, :]
+                .rearrange("p (m i) t -> p m t i", i=4),
+                in_=got("w_raw%d" % q, q)[:, c, :, part : part + W_PIECE_COLS].rearrange("p t (m i) -> p m t i", i=4),
             )
 
         def quantise_weight(q):
@@ -189,7 +179,7 @@ def tile_ta_lstmcell_v_kernel(
             nc.vector.quantize_mx(
                 out=w_codes[:, passes, :].rearrange("p c n -> p (c n)").bitcast(E4M3_X4),
                 scales=w_scales[:, passes, :].rearrange("p c n -> p (c n)"),
-                in_=got("w_grouped", q)[:].rearrange("p c n t -> p (c n t)"),
+                in_=got("w_grouped", q)[:].rearrange("p n t -> p (n t)"),
             )
 
         def multiply(n):
@@ -216,34 +206,31 @@ def tile_ta_lstmcell_v_kernel(
             if 0 <= n < count:
                 step(n)
 
-        for j in range(-3, GROUPS):
+        for j in range(-3, GROUPS + 1):
             run(load_group, j + 3)
             run(load_weight, j + 2, GATES)
             if 0 <= j < GATES:
-                regroup_weight(j, 0)
-            run(op_m1, j + 1)
+                for piece in range(W_PIECES - 1):
+                    regroup_weight(nc.scalar.copy, j, piece)
+            run(op_xn, j)
             run(op_d_o, j)
+            run(turn_cell_grads, j)
+            run(quantise_dgates, j - 1)
+            run(op_m1, j + 1)
             run(op_m2, j + 1)
-            run(op_e, j)
-            run(op_s, j + 1)
-            run(act_tc, j + 1)
-            run(op_dn, j)
+            run(cell_acts, j + 1)
             run(op_ho, j + 1)
-            run(op_d_i, j)
-            run(op_q, j + 1)
-            run(op_d_f, j)
-            run(op_pi, j + 1)
-            run(op_eg, j)
             run(op_pf, j + 1)
-            run(op_d_g, j)
-            run(gate_tanhs, j + 2)
-            run(transpose_ca, j + 2)
-            run(transpose_ghy, j + 2)
-            run(transpose_gcy, j + 1)
+            run(op_pi, j + 1)
+            run(op_q, j + 1)
             if 0 <= j < GATES:
-                regroup_weight(j, 1)
+                regroup_weight(nc.vector.tensor_copy, j, W_PIECES - 1)
+            run(op_eg, j)
+            run(op_d_i, j)
+            run(op_d_f, j)
+            run(op_d_g, j)
             run(quantise_weight, j - 1, GATES)
-            run(quantise_dgates, j)
+            run(first_acts, j + 2)
             if j >= GATES:
-                for n in range(0 if j == GATES else j, j + 1):
+                for n in range(0 if j == GATES else j - 1, j):
                     multiply(n)

@@ -11,6 +11,7 @@ U8 = mybir.dt.uint8
 E4M3_X4 = mybir.dt.float8_e4m3fn_x4
 E5M2_X4 = mybir.dt.float8_e5m2_x4
 ADD = mybir.AluOpType.add
+SUB = mybir.AluOpType.subtract
 MULT = mybir.AluOpType.mult
 TANH = mybir.ActivationFunctionType.Tanh
 SQUARE = mybir.ActivationFunctionType.Square
@@ -23,8 +24,8 @@ GATES = 4
 GATE_I, GATE_F, GATE_G, GATE_O = 0, 1, 2, 3
 HALVES = H // K_PASS
 GROUPS = (B // P) * HALVES
-W_PIECES = 4
-W_PIECE_COLS = HALVES * I_DIM // W_PIECES
+TURNED_BANKS = 6
+MULTIPLIES_A_ROUND = 2
 
 FLOPS = 2 * B * GATES * H * I_DIM
 BYTES = 4 * B * GATES * H + 4 * B * H + 2 * 2 * B * H + 2 * GATES * H * I_DIM + 4 * B * I_DIM
@@ -48,6 +49,8 @@ def tile_ta_lstmcell_v_kernel(
 
         ident_f32 = const.tile([P, P], F32)
         make_identity(nc, ident_f32[:])
+        ident_bf16 = const.tile([P, P], BF16)
+        make_identity(nc, ident_bf16[:])
         w_codes = const.tile([P, GATES * HALVES, I_DIM], U32, align_bytes=64)
         w_scales = const.tile([P, GATES * HALVES, I_DIM], U8, align_bytes=64)
 
@@ -57,18 +60,18 @@ def tile_ta_lstmcell_v_kernel(
         def hidden_cols(n, start=0):
             return slice(start + (n % HALVES) * K_PASS, start + (n % HALVES + 1) * K_PASS)
 
-        def new(pool, name, n, dtype=F32, shape=(P, K_PASS), **kw):
-            tiles[(name, n)] = pool.tile(list(shape), dtype, name=name, tag=name, **kw)
+        def new(pool, name, n, dtype=F32, shape=(P, K_PASS), tag=None, **kw):
+            tiles[(name, n)] = pool.tile(list(shape), dtype, name=name, tag=tag or name, **kw)
             return tiles[(name, n)]
 
         def got(name, n):
             return tiles[(name, n)]
 
-        def packed(flat):
-            return flat.rearrange("p (b t) -> p b t", t=PACK)
+        def packed(name, n):
+            return got(name, n)[:].rearrange("p (b t) -> p b t", t=PACK)
 
-        def turned(flat):
-            return flat.rearrange("p (t b) -> p b t", t=PACK)
+        def bank(name, n):
+            return got(name + "_t", n)[:].rearrange("p (t b) -> p b t", t=PACK)
 
         def load_group(n):
             for name, start in (("zf", GATE_F * H), ("ca", None), ("zi", GATE_I * H), ("zg", GATE_G * H), ("zo", GATE_O * H)):
@@ -85,47 +88,45 @@ def tile_ta_lstmcell_v_kernel(
                 in_=weight_ih[q * H : (q + 1) * H, :].rearrange("(c t p) n -> p c t n", t=PACK, p=P),
             )
 
-        def turn(name, n, terms, **kw):
-            bank = new(psum, name, n, **kw)
+        def turn(name, n, terms):
+            turned = new(psum, name + "_t", n, terms[0].dtype, tag="turned", bufs=TURNED_BANKS)
+            ident = ident_f32 if terms[0].dtype == F32 else ident_bf16
             for t in range(PACK):
                 block = slice(t * P, (t + 1) * P)
                 for term in terms:
                     nc.tensor.matmul(
-                        out=bank[:, block], lhsT=term[:, block], rhs=ident_f32[:], is_transpose=True,
+                        out=turned[:, block], lhsT=term[:, block], rhs=ident[:], is_transpose=True,
                         start=(term is terms[0]), stop=(term is terms[-1]),
                     )
-            return bank
 
-        def act(name, n, pool, src, func, scale=1.0):
-            nc.scalar.activation(out=new(pool, name, n)[:], in_=src[:], func=func, scale=scale)
+        def turn_one(name):
+            return lambda n: turn(name, n, [got(name, n)])
 
-        def first_acts(n):
-            act("tf", n, acts, turn("z", n, [got("zf", n)], bufs=2), TANH, 0.5)
-            turn("ca_t", n, [got("ca", n)])
-            act("ti", n, acts, turn("z", n, [got("zi", n)], bufs=2), TANH, 0.5)
-            act("g", n, acts, turn("z", n, [got("zg", n)], bufs=2), TANH)
-            act("half_g2", n, acts, got("g", n), SQUARE, math.sqrt(0.5))
-            act("to", n, acts, got("zo", n), TANH, 0.5)
-            nc.scalar.mul(out=new(acts, "neg_gcy", n)[:], in_=got("grads", n)[:, 1, :], mul=-1.0)
+        def turn_s(n):
+            turn("s", n, [got("m1", n), got("m2", n)])
 
-        def cell_acts(n):
-            act("tc", n, work, turn("s", n, [got("m1", n), got("m2", n)]), TANH, 0.5)
-            act("half_tc2", n, work, got("tc", n), SQUARE, math.sqrt(0.5))
+        def turn_gcy(n):
+            turn("gcy", n, [got("grads", n)[:, 1, :]])
 
-        def stt(out, in0, scalar, in1, op0):
-            nc.vector.scalar_tensor_tensor(out=out, in0=in0, scalar=scalar, in1=in1, op0=op0, op1=MULT)
+        def tanh_of(name, src, scale):
+            return lambda n: nc.scalar.activation(out=new(acts, name, n)[:], in_=got(src, n)[:], func=TANH, scale=scale)
+
+        def act_half_g2(n):
+            nc.scalar.activation(out=new(acts, "half_g2", n)[:], in_=got("g", n)[:], func=SQUARE, scale=math.sqrt(0.5))
+
+        def act_tc(n):
+            new(work, "tc", n)
+            nc.scalar.activation(out=packed("tc", n), in_=bank("s", n), func=TANH, scale=0.5)
+            nc.scalar.activation(out=new(work, "tc2", n)[:], in_=got("tc", n)[:], func=SQUARE)
+
+        def stt(out, in0, scalar, in1, op0, op1=MULT):
+            nc.vector.scalar_tensor_tensor(out=out, in0=in0, scalar=scalar, in1=in1, op0=op0, op1=op1)
 
         def op_m1(n):
-            stt(new(work, "m1", n)[:], got("tf", n)[:], 1.0, got("ca_t", n)[:], ADD)
+            stt(new(work, "m1", n)[:], got("tf", n)[:], 1.0, got("ca", n)[:], ADD)
 
         def op_m2(n):
             stt(new(work, "m2", n)[:], got("ti", n)[:], 1.0, got("g", n)[:], ADD)
-
-        def op_pf(n):
-            stt(new(work, "pf", n)[:], got("tf", n)[:], -1.0, got("m1", n)[:], ADD)
-
-        def op_pi(n):
-            stt(new(work, "pi", n)[:], got("ti", n)[:], -1.0, got("m2", n)[:], ADD)
 
         def op_ho(n):
             stt(new(work, "ho", n)[:], got("to", n)[:], 1.0, got("grads", n)[:, 0, :], ADD)
@@ -133,29 +134,39 @@ def tile_ta_lstmcell_v_kernel(
         def op_q(n):
             stt(new(work, "q", n)[:], got("to", n)[:], -1.0, got("ho", n)[:], ADD)
 
-        def op_xn(n):
-            stt(new(work, "xn", n)[:], got("half_tc2", n)[:], -0.5, got("ho", n)[:], ADD)
+        def op_pf(n):
+            stt(new(work, "pf", n)[:], got("tf", n)[:], -1.0, got("m1", n)[:], ADD)
+
+        def op_pi(n):
+            stt(new(work, "pi", n)[:], got("ti", n)[:], -1.0, got("m2", n)[:], ADD)
+
+        def dgate(n, q):
+            return got("dq", n)[:, q, :].rearrange("p (b t) -> p b t", t=PACK)
 
         def op_d_o(n):
-            stt(new(work, "d_o", n)[:], got("q", n)[:], -0.25, got("tc", n)[:], MULT)
+            new(work, "dq", n, BF16, (P, GATES, K_PASS), align_bytes=64)
+            stt(dgate(n, GATE_O), bank("q", n), -0.25, packed("tc", n), MULT)
 
-        def turn_cell_grads(n):
-            turn("dn", n, [got("xn", n), got("neg_gcy", n)])
-            d_o_t = turn("d_o_t", n, [got("d_o", n)])
-            dq = new(work, "dq", n, BF16, (P, GATES, K_PASS), align_bytes=64)
-            nc.scalar.copy(out=packed(dq[:, GATE_O, :]), in_=turned(d_o_t[:]))
+        def op_e(n):
+            new(work, "e", n)
+            stt(packed("e", n), packed("tc2", n), -1.0, bank("ho", n), ADD)
+
+        def op_dn(n):
+            new(work, "dn", n)
+            stt(packed("dn", n), packed("e", n), 0.5, bank("gcy", n), MULT, SUB)
 
         def op_eg(n):
-            stt(packed(new(work, "eg", n)[:]), turned(got("half_g2", n)[:]), -0.5, turned(got("dn", n)[:]), ADD)
+            new(work, "eg", n)
+            stt(packed("eg", n), bank("half_g2", n), -0.5, packed("dn", n), ADD)
 
         def op_d_i(n):
-            stt(packed(got("dq", n)[:, GATE_I, :]), turned(got("pi", n)[:]), 0.25, turned(got("dn", n)[:]), MULT)
+            stt(dgate(n, GATE_I), bank("pi", n), 0.25, packed("dn", n), MULT)
 
         def op_d_f(n):
-            stt(packed(got("dq", n)[:, GATE_F, :]), turned(got("pf", n)[:]), 0.25, turned(got("dn", n)[:]), MULT)
+            stt(dgate(n, GATE_F), bank("pf", n), 0.25, packed("dn", n), MULT)
 
         def op_d_g(n):
-            stt(packed(got("dq", n)[:, GATE_G, :]), turned(got("ti", n)[:]), 1.0, packed(got("eg", n)[:]), ADD)
+            stt(dgate(n, GATE_G), bank("ti", n), 1.0, packed("eg", n), ADD)
 
         def quantise_dgates(n):
             nc.vector.quantize_mx(
@@ -164,14 +175,12 @@ def tile_ta_lstmcell_v_kernel(
                 in_=got("dq", n)[:].rearrange("p q c -> p (q c)"),
             )
 
-        def regroup_weight(copy, q, piece):
-            if piece == 0:
-                new(work, "w_grouped", q, BF16, (P, HALVES * I_DIM, PACK), align_bytes=64)
-            c, part = divmod(piece * W_PIECE_COLS, I_DIM)
-            copy(
-                out=got("w_grouped", q)[:, piece * W_PIECE_COLS : (piece + 1) * W_PIECE_COLS, :]
-                .rearrange("p (m i) t -> p m t i", i=4),
-                in_=got("w_raw%d" % q, q)[:, c, :, part : part + W_PIECE_COLS].rearrange("p t (m i) -> p m t i", i=4),
+        def regroup_weight(q, c):
+            if c == 0:
+                new(work, "w_grouped", q, BF16, (P, HALVES, I_DIM, PACK), align_bytes=64)
+            nc.scalar.copy(
+                out=got("w_grouped", q)[:, c].rearrange("p (m i) t -> p m t i", i=4),
+                in_=got("w_raw%d" % q, q)[:, c].rearrange("p t (m i) -> p m t i", i=4),
             )
 
         def quantise_weight(q):
@@ -179,7 +188,7 @@ def tile_ta_lstmcell_v_kernel(
             nc.vector.quantize_mx(
                 out=w_codes[:, passes, :].rearrange("p c n -> p (c n)").bitcast(E4M3_X4),
                 scales=w_scales[:, passes, :].rearrange("p c n -> p (c n)"),
-                in_=got("w_grouped", q)[:].rearrange("p n t -> p (n t)"),
+                in_=got("w_grouped", q)[:].rearrange("p c n t -> p (c n t)"),
             )
 
         def multiply(n):
@@ -206,31 +215,44 @@ def tile_ta_lstmcell_v_kernel(
             if 0 <= n < count:
                 step(n)
 
+        multiplied = 0
         for j in range(-3, GROUPS + 1):
             run(load_group, j + 3)
             run(load_weight, j + 2, GATES)
             if 0 <= j < GATES:
-                for piece in range(W_PIECES - 1):
-                    regroup_weight(nc.scalar.copy, j, piece)
-            run(op_xn, j)
-            run(op_d_o, j)
-            run(turn_cell_grads, j)
-            run(quantise_dgates, j - 1)
+                regroup_weight(j, 0)
+            run(tanh_of("tf", "zf", 0.5), j + 2)
+            run(tanh_of("ti", "zi", 0.5), j + 2)
+            run(tanh_of("g", "zg", 1.0), j + 2)
+            run(turn_one("half_g2"), j)
+            run(turn_one("pi"), j)
             run(op_m1, j + 1)
+            run(quantise_dgates, j - 1)
+            run(op_d_o, j)
             run(op_m2, j + 1)
-            run(cell_acts, j + 1)
+            run(turn_s, j + 1)
+            run(act_tc, j + 1)
+            run(op_e, j)
+            run(turn_one("ti"), j)
+            run(turn_one("pf"), j)
+            run(tanh_of("to", "zo", 0.5), j + 2)
+            run(act_half_g2, j + 2)
             run(op_ho, j + 1)
-            run(op_pf, j + 1)
-            run(op_pi, j + 1)
+            run(op_dn, j)
+            run(turn_one("ho"), j + 1)
             run(op_q, j + 1)
-            if 0 <= j < GATES:
-                regroup_weight(nc.vector.tensor_copy, j, W_PIECES - 1)
             run(op_eg, j)
+            run(turn_one("q"), j + 1)
+            run(op_pf, j + 1)
             run(op_d_i, j)
-            run(op_d_f, j)
+            run(turn_gcy, j + 1)
+            run(op_pi, j + 1)
             run(op_d_g, j)
+            run(op_d_f, j)
+            if 0 <= j < GATES:
+                regroup_weight(j, 1)
             run(quantise_weight, j - 1, GATES)
-            run(first_acts, j + 2)
             if j >= GATES:
-                for n in range(0 if j == GATES else j - 1, j):
+                for n in range(multiplied, min(multiplied + MULTIPLIES_A_ROUND, j)):
                     multiply(n)
+                    multiplied = n + 1

@@ -25,7 +25,7 @@ GATE_I, GATE_F, GATE_G, GATE_O = 0, 1, 2, 3
 HALVES = H // K_PASS
 GROUPS = (B // P) * HALVES
 TURNED_BANKS = 6
-MULTIPLIES_A_ROUND = 2
+GATE_ORDER = (GATE_O, GATE_I, GATE_F, GATE_G)
 
 FLOPS = 2 * B * GATES * H * I_DIM
 BYTES = 4 * B * GATES * H + 4 * B * H + 2 * 2 * B * H + 2 * GATES * H * I_DIM + 4 * B * I_DIM
@@ -141,7 +141,7 @@ def tile_ta_lstmcell_v_kernel(
             stt(new(work, "pi", n)[:], got("ti", n)[:], -1.0, got("m2", n)[:], ADD)
 
         def dgate(n, q):
-            return got("dq", n)[:, q, :].rearrange("p (b t) -> p b t", t=PACK)
+            return got("dq", n)[:, GATE_ORDER.index(q), :].rearrange("p (b t) -> p b t", t=PACK)
 
         def op_d_o(n):
             new(work, "dq", n, BF16, (P, GATES, K_PASS), align_bytes=64)
@@ -168,12 +168,22 @@ def tile_ta_lstmcell_v_kernel(
         def op_d_g(n):
             stt(dgate(n, GATE_G), bank("ti", n), 1.0, packed("eg", n), ADD)
 
-        def quantise_dgates(n):
+        def quantise_dgates(n, first, count):
+            if first == 0:
+                new(codes, "d_codes", n, U32, (P, GATES * P), align_bytes=64)
+                new(codes, "d_scales", n, U8, (P, GATES * P), align_bytes=64)
+            words = slice(first * P, (first + count) * P)
             nc.vector.quantize_mx(
-                out=new(codes, "d_codes", n, U32, (P, GATES * P), align_bytes=64)[:].bitcast(E5M2_X4),
-                scales=new(codes, "d_scales", n, U8, (P, GATES * P), align_bytes=64)[:],
-                in_=got("dq", n)[:].rearrange("p q c -> p (q c)"),
+                out=got("d_codes", n)[:, words].bitcast(E5M2_X4),
+                scales=got("d_scales", n)[:, words],
+                in_=got("dq", n)[:, first : first + count, :].rearrange("p q c -> p (q c)"),
             )
+
+        def quantise_first_two(n):
+            quantise_dgates(n, 0, 2)
+
+        def quantise_last_two(n):
+            quantise_dgates(n, 2, 2)
 
         def regroup_weight(q, c):
             if c == 0:
@@ -196,15 +206,15 @@ def tile_ta_lstmcell_v_kernel(
             if half == 0:
                 new(psum, "acc", b_tile, F32, (P, I_DIM), bufs=2)
             acc = got("acc", b_tile)
-            for q in range(GATES):
+            for place, q in enumerate(GATE_ORDER):
                 nc.tensor.matmul_mx(
                     out=acc[:],
-                    lhsT=got("d_codes", n)[:, q * P : (q + 1) * P].bitcast(E5M2_X4),
-                    lhsT_scale=got("d_scales", n)[:, q * P : (q + 1) * P],
+                    lhsT=got("d_codes", n)[:, place * P : (place + 1) * P].bitcast(E5M2_X4),
+                    lhsT_scale=got("d_scales", n)[:, place * P : (place + 1) * P],
                     rhs=w_codes[:, q * HALVES + half, :].bitcast(E4M3_X4),
                     rhs_scale=w_scales[:, q * HALVES + half, :],
-                    start=(half == 0 and q == 0),
-                    stop=(half == HALVES - 1 and q == GATES - 1),
+                    start=(half == 0 and place == 0),
+                    stop=(half == HALVES - 1 and place == GATES - 1),
                 )
             if half == HALVES - 1:
                 result = work.tile([P, I_DIM], F32)
@@ -215,7 +225,6 @@ def tile_ta_lstmcell_v_kernel(
             if 0 <= n < count:
                 step(n)
 
-        multiplied = 0
         for j in range(-3, GROUPS + 1):
             run(load_group, j + 3)
             run(load_weight, j + 2, GATES)
@@ -224,35 +233,35 @@ def tile_ta_lstmcell_v_kernel(
             run(tanh_of("tf", "zf", 0.5), j + 2)
             run(tanh_of("ti", "zi", 0.5), j + 2)
             run(tanh_of("g", "zg", 1.0), j + 2)
-            run(turn_one("half_g2"), j)
-            run(turn_one("pi"), j)
             run(op_m1, j + 1)
-            run(quantise_dgates, j - 1)
+            run(quantise_last_two, j - 1)
             run(op_d_o, j)
             run(op_m2, j + 1)
             run(turn_s, j + 1)
             run(act_tc, j + 1)
             run(op_e, j)
-            run(turn_one("ti"), j)
-            run(turn_one("pf"), j)
             run(tanh_of("to", "zo", 0.5), j + 2)
             run(act_half_g2, j + 2)
             run(op_ho, j + 1)
             run(op_dn, j)
-            run(turn_one("ho"), j + 1)
+            run(turn_one("ti"), j)
+            run(turn_one("pf"), j)
+            run(turn_gcy, j + 1)
             run(op_q, j + 1)
             run(op_eg, j)
-            run(turn_one("q"), j + 1)
             run(op_pf, j + 1)
             run(op_d_i, j)
-            run(turn_gcy, j + 1)
+            run(turn_one("ho"), j + 1)
+            run(turn_one("q"), j + 1)
             run(op_pi, j + 1)
-            run(op_d_g, j)
+            run(turn_one("pi"), j + 1)
+            run(quantise_first_two, j)
             run(op_d_f, j)
+            run(op_d_g, j)
+            run(turn_one("half_g2"), j + 1)
             if 0 <= j < GATES:
                 regroup_weight(j, 1)
             run(quantise_weight, j - 1, GATES)
             if j >= GATES:
-                for n in range(multiplied, min(multiplied + MULTIPLIES_A_ROUND, j)):
+                for n in range(0 if j == GATES else j - 1, j):
                     multiply(n)
-                    multiplied = n + 1

@@ -11,7 +11,6 @@ U8 = mybir.dt.uint8
 E4M3_X4 = mybir.dt.float8_e4m3fn_x4
 E5M2_X4 = mybir.dt.float8_e5m2_x4
 ADD = mybir.AluOpType.add
-SUB = mybir.AluOpType.subtract
 MULT = mybir.AluOpType.mult
 TANH = mybir.ActivationFunctionType.Tanh
 SQUARE = mybir.ActivationFunctionType.Square
@@ -24,8 +23,8 @@ GATES = 4
 GATE_I, GATE_F, GATE_G, GATE_O = 0, 1, 2, 3
 HALVES = H // K_PASS
 GROUPS = (B // P) * HALVES
-TURNED_BANKS = 6
-GATE_ORDER = (GATE_O, GATE_I, GATE_F, GATE_G)
+W_PIECES = 4
+W_PIECE_COLS = HALVES * I_DIM // W_PIECES
 
 FLOPS = 2 * B * GATES * H * I_DIM
 BYTES = 4 * B * GATES * H + 4 * B * H + 2 * 2 * B * H + 2 * GATES * H * I_DIM + 4 * B * I_DIM
@@ -88,8 +87,10 @@ def tile_ta_lstmcell_v_kernel(
                 in_=weight_ih[q * H : (q + 1) * H, :].rearrange("(c t p) n -> p c t n", t=PACK, p=P),
             )
 
+        bank_of = {"s": "s", "hn": "hn_pf", "pf": "hn_pf", "q": "q_ti", "ti": "q_ti", "gcy": "gcy", "half_g2": "half_g2", "pi": "pi"}
+
         def turn(name, n, terms):
-            turned = new(psum, name + "_t", n, terms[0].dtype, tag="turned", bufs=TURNED_BANKS)
+            turned = new(psum, name + "_t", n, terms[0].dtype, tag=bank_of[name])
             ident = ident_f32 if terms[0].dtype == F32 else ident_bf16
             for t in range(PACK):
                 block = slice(t * P, (t + 1) * P)
@@ -99,11 +100,8 @@ def tile_ta_lstmcell_v_kernel(
                         start=(term is terms[0]), stop=(term is terms[-1]),
                     )
 
-        def turn_one(name):
-            return lambda n: turn(name, n, [got(name, n)])
-
-        def turn_s(n):
-            turn("s", n, [got("m1", n), got("m2", n)])
+        def turn_sum(name, *term_names):
+            return lambda n: turn(name, n, [got(term, n) for term in term_names])
 
         def turn_gcy(n):
             turn("gcy", n, [got("grads", n)[:, 1, :]])
@@ -116,81 +114,73 @@ def tile_ta_lstmcell_v_kernel(
 
         def act_tc(n):
             new(work, "tc", n)
-            nc.scalar.activation(out=packed("tc", n), in_=bank("s", n), func=TANH, scale=0.5)
+            nc.scalar.activation(out=packed("tc", n), in_=bank("s", n), func=TANH, scale=-0.5)
             nc.scalar.activation(out=new(work, "tc2", n)[:], in_=got("tc", n)[:], func=SQUARE)
 
         def stt(out, in0, scalar, in1, op0, op1=MULT):
             nc.vector.scalar_tensor_tensor(out=out, in0=in0, scalar=scalar, in1=in1, op0=op0, op1=op1)
 
         def op_m1(n):
-            stt(new(work, "m1", n)[:], got("tf", n)[:], 1.0, got("ca", n)[:], ADD)
+            stt(new(work, "m1", n)[:], got("tf", n)[:], -1.0, got("ca", n)[:], ADD)
 
         def op_m2(n):
-            stt(new(work, "m2", n)[:], got("ti", n)[:], 1.0, got("g", n)[:], ADD)
+            stt(new(work, "m2", n)[:], got("ti", n)[:], -1.0, got("g", n)[:], ADD)
 
-        def op_ho(n):
-            stt(new(work, "ho", n)[:], got("to", n)[:], 1.0, got("grads", n)[:, 0, :], ADD)
-
-        def op_q(n):
-            stt(new(work, "q", n)[:], got("to", n)[:], -1.0, got("ho", n)[:], ADD)
-
-        def op_pf(n):
-            stt(new(work, "pf", n)[:], got("tf", n)[:], -1.0, got("m1", n)[:], ADD)
+        def op_hn(n):
+            stt(new(work, "hn", n)[:], got("to", n)[:], -1.0, got("grads", n)[:, 0, :], ADD)
 
         def op_pi(n):
-            stt(new(work, "pi", n)[:], got("ti", n)[:], -1.0, got("m2", n)[:], ADD)
+            stt(new(work, "pi", n)[:], got("ti", n)[:], 1.0, got("m2", n)[:], ADD)
+
+        def op_tf_m1(n):
+            nc.gpsimd.tensor_tensor(out=new(work, "tf_m1", n)[:], in0=got("tf", n)[:], in1=got("m1", n)[:], op=MULT)
+
+        def op_to_hn(n):
+            nc.gpsimd.tensor_tensor(out=new(work, "to_hn", n)[:], in0=got("to", n)[:], in1=got("hn", n)[:], op=MULT)
 
         def dgate(n, q):
-            return got("dq", n)[:, GATE_ORDER.index(q), :].rearrange("p (b t) -> p b t", t=PACK)
+            return got("dq", n)[:, q, :].rearrange("p (b t) -> p b t", t=PACK)
+
+        def op_e(n):
+            new(work, "e", n)
+            stt(packed("e", n), packed("tc2", n), -1.0, bank("hn", n), ADD)
 
         def op_d_o(n):
             new(work, "dq", n, BF16, (P, GATES, K_PASS), align_bytes=64)
             stt(dgate(n, GATE_O), bank("q", n), -0.25, packed("tc", n), MULT)
 
-        def op_e(n):
-            new(work, "e", n)
-            stt(packed("e", n), packed("tc2", n), -1.0, bank("ho", n), ADD)
-
-        def op_dn(n):
-            new(work, "dn", n)
-            stt(packed("dn", n), packed("e", n), 0.5, bank("gcy", n), MULT, SUB)
+        def op_d_cy(n):
+            new(work, "d_cy", n)
+            stt(packed("d_cy", n), packed("e", n), 0.5, bank("gcy", n), MULT, ADD)
 
         def op_eg(n):
             new(work, "eg", n)
-            stt(packed("eg", n), bank("half_g2", n), -0.5, packed("dn", n), ADD)
+            stt(packed("eg", n), bank("half_g2", n), -0.5, packed("d_cy", n), ADD)
 
         def op_d_i(n):
-            stt(dgate(n, GATE_I), bank("pi", n), 0.25, packed("dn", n), MULT)
+            stt(dgate(n, GATE_I), bank("pi", n), -0.25, packed("d_cy", n), MULT)
 
         def op_d_f(n):
-            stt(dgate(n, GATE_F), bank("pf", n), 0.25, packed("dn", n), MULT)
+            stt(dgate(n, GATE_F), bank("pf", n), -0.25, packed("d_cy", n), MULT)
 
         def op_d_g(n):
-            stt(dgate(n, GATE_G), bank("ti", n), 1.0, packed("eg", n), ADD)
+            stt(dgate(n, GATE_G), bank("ti", n), -1.0, packed("eg", n), ADD)
 
-        def quantise_dgates(n, first, count):
-            if first == 0:
-                new(codes, "d_codes", n, U32, (P, GATES * P), align_bytes=64)
-                new(codes, "d_scales", n, U8, (P, GATES * P), align_bytes=64)
-            words = slice(first * P, (first + count) * P)
+        def quantise_dgates(n):
             nc.vector.quantize_mx(
-                out=got("d_codes", n)[:, words].bitcast(E5M2_X4),
-                scales=got("d_scales", n)[:, words],
-                in_=got("dq", n)[:, first : first + count, :].rearrange("p q c -> p (q c)"),
+                out=new(codes, "d_codes", n, U32, (P, GATES * P), align_bytes=64)[:].bitcast(E5M2_X4),
+                scales=new(codes, "d_scales", n, U8, (P, GATES * P), align_bytes=64)[:],
+                in_=got("dq", n)[:].rearrange("p q c -> p (q c)"),
             )
 
-        def quantise_first_two(n):
-            quantise_dgates(n, 0, 2)
-
-        def quantise_last_two(n):
-            quantise_dgates(n, 2, 2)
-
-        def regroup_weight(q, c):
-            if c == 0:
-                new(work, "w_grouped", q, BF16, (P, HALVES, I_DIM, PACK), align_bytes=64)
-            nc.scalar.copy(
-                out=got("w_grouped", q)[:, c].rearrange("p (m i) t -> p m t i", i=4),
-                in_=got("w_raw%d" % q, q)[:, c].rearrange("p t (m i) -> p m t i", i=4),
+        def regroup_weight(copy, q, piece):
+            if piece == 0:
+                new(work, "w_grouped", q, BF16, (P, HALVES * I_DIM, PACK), align_bytes=64)
+            c, part = divmod(piece * W_PIECE_COLS, I_DIM)
+            copy(
+                out=got("w_grouped", q)[:, piece * W_PIECE_COLS : (piece + 1) * W_PIECE_COLS, :]
+                .rearrange("p (m i) t -> p m t i", i=4),
+                in_=got("w_raw%d" % q, q)[:, c, :, part : part + W_PIECE_COLS].rearrange("p t (m i) -> p m t i", i=4),
             )
 
         def quantise_weight(q):
@@ -198,7 +188,7 @@ def tile_ta_lstmcell_v_kernel(
             nc.vector.quantize_mx(
                 out=w_codes[:, passes, :].rearrange("p c n -> p (c n)").bitcast(E4M3_X4),
                 scales=w_scales[:, passes, :].rearrange("p c n -> p (c n)"),
-                in_=got("w_grouped", q)[:].rearrange("p c n t -> p (c n t)"),
+                in_=got("w_grouped", q)[:].rearrange("p n t -> p (n t)"),
             )
 
         def multiply(n):
@@ -206,15 +196,15 @@ def tile_ta_lstmcell_v_kernel(
             if half == 0:
                 new(psum, "acc", b_tile, F32, (P, I_DIM), bufs=2)
             acc = got("acc", b_tile)
-            for place, q in enumerate(GATE_ORDER):
+            for q in range(GATES):
                 nc.tensor.matmul_mx(
                     out=acc[:],
-                    lhsT=got("d_codes", n)[:, place * P : (place + 1) * P].bitcast(E5M2_X4),
-                    lhsT_scale=got("d_scales", n)[:, place * P : (place + 1) * P],
+                    lhsT=got("d_codes", n)[:, q * P : (q + 1) * P].bitcast(E5M2_X4),
+                    lhsT_scale=got("d_scales", n)[:, q * P : (q + 1) * P],
                     rhs=w_codes[:, q * HALVES + half, :].bitcast(E4M3_X4),
                     rhs_scale=w_scales[:, q * HALVES + half, :],
-                    start=(half == 0 and place == 0),
-                    stop=(half == HALVES - 1 and place == GATES - 1),
+                    start=(half == 0 and q == 0),
+                    stop=(half == HALVES - 1 and q == GATES - 1),
                 )
             if half == HALVES - 1:
                 result = work.tile([P, I_DIM], F32)
@@ -229,38 +219,43 @@ def tile_ta_lstmcell_v_kernel(
             run(load_group, j + 3)
             run(load_weight, j + 2, GATES)
             if 0 <= j < GATES:
-                regroup_weight(j, 0)
-            run(tanh_of("tf", "zf", 0.5), j + 2)
-            run(tanh_of("ti", "zi", 0.5), j + 2)
+                for piece in range(W_PIECES - 1):
+                    regroup_weight(nc.scalar.copy, j, piece)
+            run(tanh_of("tf", "zf", -0.5), j + 2)
+            run(tanh_of("ti", "zi", -0.5), j + 2)
             run(tanh_of("g", "zg", 1.0), j + 2)
+
+            run(quantise_dgates, j - 1)
             run(op_m1, j + 1)
-            run(quantise_last_two, j - 1)
-            run(op_d_o, j)
+            run(op_tf_m1, j + 1)
             run(op_m2, j + 1)
-            run(turn_s, j + 1)
+            run(turn_sum("s", "m1", "m2"), j + 1)
             run(act_tc, j + 1)
+
             run(op_e, j)
-            run(tanh_of("to", "zo", 0.5), j + 2)
-            run(act_half_g2, j + 2)
-            run(op_ho, j + 1)
-            run(op_dn, j)
-            run(turn_one("ti"), j)
-            run(turn_one("pf"), j)
+            run(turn_sum("pf", "tf_m1", "m1"), j)
+            run(op_d_o, j)
+            run(turn_sum("ti", "ti"), j)
+            run(op_d_cy, j)
             run(turn_gcy, j + 1)
-            run(op_q, j + 1)
-            run(op_eg, j)
-            run(op_pf, j + 1)
-            run(op_d_i, j)
-            run(turn_one("ho"), j + 1)
-            run(turn_one("q"), j + 1)
+            run(tanh_of("to", "zo", -0.5), j + 2)
+            run(act_half_g2, j + 2)
+
+            run(op_hn, j + 1)
+            run(op_to_hn, j + 1)
             run(op_pi, j + 1)
-            run(turn_one("pi"), j + 1)
-            run(quantise_first_two, j)
-            run(op_d_f, j)
-            run(op_d_g, j)
-            run(turn_one("half_g2"), j + 1)
             if 0 <= j < GATES:
-                regroup_weight(j, 1)
+                regroup_weight(nc.vector.tensor_copy, j, W_PIECES - 1)
+
+            run(op_eg, j)
+            run(turn_sum("half_g2", "half_g2"), j + 1)
+            run(op_d_i, j)
+            run(turn_sum("pi", "pi"), j + 1)
+            run(op_d_f, j)
+            run(turn_sum("hn", "hn"), j + 1)
+            run(op_d_g, j)
+            run(turn_sum("q", "to_hn", "hn"), j + 1)
+
             run(quantise_weight, j - 1, GATES)
             if j >= GATES:
                 for n in range(0 if j == GATES else j - 1, j):

@@ -1,4 +1,3 @@
-import math
 from contextlib import ExitStack
 
 import concourse.mybir as mybir
@@ -13,6 +12,7 @@ E5M2_X4 = mybir.dt.float8_e5m2_x4
 ADD = mybir.AluOpType.add
 MULT = mybir.AluOpType.mult
 TANH = mybir.ActivationFunctionType.Tanh
+SIGMOID = mybir.ActivationFunctionType.Sigmoid
 SQUARE = mybir.ActivationFunctionType.Square
 
 B, I_DIM, H = 512, 512, 1024
@@ -21,6 +21,7 @@ PACK = 4
 K_PASS = P * PACK
 GATES = 4
 GATE_I, GATE_F, GATE_G, GATE_O = 0, 1, 2, 3
+SLOT = {GATE_O: 0, GATE_F: 1, GATE_I: 2, GATE_G: 3}
 HALVES = H // K_PASS
 GROUPS = (B // P) * HALVES
 W_PIECES = 4
@@ -73,7 +74,7 @@ def tile_ta_lstmcell_v_kernel(
             return got(name + "_t", n)[:].rearrange("p (t b) -> p b t", t=PACK)
 
         def load_group(n):
-            for name, start in (("zf", GATE_F * H), ("ca", None), ("zi", GATE_I * H), ("zg", GATE_G * H), ("zo", GATE_O * H)):
+            for name, start in (("zi", GATE_I * H), ("zg", GATE_G * H), ("zf", GATE_F * H), ("ca", None), ("zo", GATE_O * H)):
                 src = cx_adj[batch_rows(n), hidden_cols(n)] if start is None else gates[batch_rows(n), hidden_cols(n, start)]
                 nc.sync.dma_start(out=new(raw, name, n)[:], in_=src)
             nc.sync.dma_start(
@@ -87,7 +88,7 @@ def tile_ta_lstmcell_v_kernel(
                 in_=weight_ih[q * H : (q + 1) * H, :].rearrange("(c t p) n -> p c t n", t=PACK, p=P),
             )
 
-        bank_of = {"s": "s", "hn": "hn_pf", "pf": "hn_pf", "q": "q_ti", "ti": "q_ti", "gcy": "gcy", "half_g2": "half_g2", "pi": "pi"}
+        bank_of = {"s": "s", "hn": "hn_pf", "pf": "hn_pf", "q": "q", "ib": "ib", "gcy": "gcy_gib", "gib": "gcy_gib", "g2": "g2"}
 
         def turn(name, n, terms):
             turned = new(psum, name + "_t", n, terms[0].dtype, tag=bank_of[name])
@@ -106,71 +107,69 @@ def tile_ta_lstmcell_v_kernel(
         def turn_gcy(n):
             turn("gcy", n, [got("grads", n)[:, 1, :]])
 
-        def tanh_of(name, src, scale):
-            return lambda n: nc.scalar.activation(out=new(acts, name, n)[:], in_=got(src, n)[:], func=TANH, scale=scale)
-
-        def act_half_g2(n):
-            nc.scalar.activation(out=new(acts, "half_g2", n)[:], in_=got("g", n)[:], func=SQUARE, scale=math.sqrt(0.5))
+        def act(name, src, func, scale=1.0):
+            return lambda n: nc.scalar.activation(out=new(acts, name, n)[:], in_=got(src, n)[:], func=func, scale=scale)
 
         def act_tc(n):
             new(work, "tc", n)
-            nc.scalar.activation(out=packed("tc", n), in_=bank("s", n), func=TANH, scale=-0.5)
+            nc.scalar.activation(out=packed("tc", n), in_=bank("s", n), func=TANH, scale=-1.0)
             nc.scalar.activation(out=new(work, "tc2", n)[:], in_=got("tc", n)[:], func=SQUARE)
 
         def stt(out, in0, scalar, in1, op0, op1=MULT):
             nc.vector.scalar_tensor_tensor(out=out, in0=in0, scalar=scalar, in1=in1, op0=op0, op1=op1)
 
         def op_m1(n):
-            stt(new(work, "m1", n)[:], got("tf", n)[:], -1.0, got("ca", n)[:], ADD)
+            stt(new(work, "m1", n)[:], got("fb", n)[:], -1.0, got("ca", n)[:], ADD)
 
         def op_m2(n):
-            stt(new(work, "m2", n)[:], got("ti", n)[:], -1.0, got("g", n)[:], ADD)
+            stt(new(work, "m2", n)[:], got("ib", n)[:], -1.0, got("g", n)[:], ADD)
 
         def op_hn(n):
-            stt(new(work, "hn", n)[:], got("to", n)[:], -1.0, got("grads", n)[:, 0, :], ADD)
+            stt(new(work, "hn", n)[:], got("ob", n)[:], -1.0, got("grads", n)[:, 0, :], ADD)
 
-        def op_pi(n):
-            stt(new(work, "pi", n)[:], got("ti", n)[:], 1.0, got("m2", n)[:], ADD)
+        def op_pf(n):
+            nc.gpsimd.tensor_tensor(out=new(work, "pf", n)[:], in0=got("fb", n)[:], in1=got("m1", n)[:], op=MULT)
 
-        def op_tf_m1(n):
-            nc.gpsimd.tensor_tensor(out=new(work, "tf_m1", n)[:], in0=got("tf", n)[:], in1=got("m1", n)[:], op=MULT)
-
-        def op_to_hn(n):
-            nc.gpsimd.tensor_tensor(out=new(work, "to_hn", n)[:], in0=got("to", n)[:], in1=got("hn", n)[:], op=MULT)
+        def op_q(n):
+            nc.gpsimd.tensor_tensor(out=new(work, "q", n)[:], in0=got("ob", n)[:], in1=got("hn", n)[:], op=MULT)
 
         def dgate(n, q):
-            return got("dq", n)[:, q, :].rearrange("p (b t) -> p b t", t=PACK)
+            return got("dq", n)[:, SLOT[q], :].rearrange("p (b t) -> p b t", t=PACK)
 
         def op_e(n):
             new(work, "e", n)
             stt(packed("e", n), packed("tc2", n), -1.0, bank("hn", n), ADD)
 
         def op_d_o(n):
-            new(work, "dq", n, BF16, (P, GATES, K_PASS), align_bytes=64)
-            stt(dgate(n, GATE_O), bank("q", n), -0.25, packed("tc", n), MULT)
+            stt(dgate(n, GATE_O), bank("q", n), -1.0, packed("tc", n), MULT)
 
         def op_d_cy(n):
             new(work, "d_cy", n)
-            stt(packed("d_cy", n), packed("e", n), 0.5, bank("gcy", n), MULT, ADD)
+            nc.vector.tensor_tensor(out=packed("d_cy", n), in0=packed("e", n), in1=bank("gcy", n), op=ADD)
 
-        def op_eg(n):
-            new(work, "eg", n)
-            stt(packed("eg", n), bank("half_g2", n), -0.5, packed("d_cy", n), ADD)
-
-        def op_d_i(n):
-            stt(dgate(n, GATE_I), bank("pi", n), -0.25, packed("d_cy", n), MULT)
+        def op_i_d(n):
+            new(work, "dq", n, BF16, (P, GATES, K_PASS), align_bytes=64)
+            new(work, "i_d", n)
+            stt(packed("i_d", n), bank("ib", n), -1.0, packed("d_cy", n), ADD)
 
         def op_d_f(n):
-            stt(dgate(n, GATE_F), bank("pf", n), -0.25, packed("d_cy", n), MULT)
+            stt(dgate(n, GATE_F), bank("pf", n), -1.0, packed("d_cy", n), MULT)
+
+        def op_d_i(n):
+            stt(dgate(n, GATE_I), bank("gib", n), -1.0, packed("i_d", n), MULT)
 
         def op_d_g(n):
-            stt(dgate(n, GATE_G), bank("ti", n), -1.0, packed("eg", n), ADD)
+            stt(dgate(n, GATE_G), bank("g2", n), -1.0, packed("i_d", n), ADD)
 
-        def quantise_dgates(n):
+        def quantise_dgates(n, first=0, last=GATES):
+            if first == 0:
+                new(codes, "d_codes", n, U32, (P, GATES * P), align_bytes=64)
+                new(codes, "d_scales", n, U8, (P, GATES * P), align_bytes=64)
+            cols = slice(first * P, last * P)
             nc.vector.quantize_mx(
-                out=new(codes, "d_codes", n, U32, (P, GATES * P), align_bytes=64)[:].bitcast(E5M2_X4),
-                scales=new(codes, "d_scales", n, U8, (P, GATES * P), align_bytes=64)[:],
-                in_=got("dq", n)[:].rearrange("p q c -> p (q c)"),
+                out=got("d_codes", n)[:, cols].bitcast(E5M2_X4),
+                scales=got("d_scales", n)[:, cols],
+                in_=got("dq", n)[:, first:last, :].rearrange("p q c -> p (q c)"),
             )
 
         def regroup_weight(copy, q, piece):
@@ -191,72 +190,102 @@ def tile_ta_lstmcell_v_kernel(
                 in_=got("w_grouped", q)[:].rearrange("p n t -> p (n t)"),
             )
 
-        def multiply(n):
+        passes_done = {}
+
+        def multiply(n, gate_list=tuple(SLOT)):
             b_tile, half = divmod(n, HALVES)
-            if half == 0:
+            if b_tile not in passes_done:
                 new(psum, "acc", b_tile, F32, (P, I_DIM), bufs=2)
-            acc = got("acc", b_tile)
-            for q in range(GATES):
+                passes_done[b_tile] = 0
+            for q in gate_list:
+                passes_done[b_tile] += 1
+                words = slice(SLOT[q] * P, (SLOT[q] + 1) * P)
                 nc.tensor.matmul_mx(
-                    out=acc[:],
-                    lhsT=got("d_codes", n)[:, q * P : (q + 1) * P].bitcast(E5M2_X4),
-                    lhsT_scale=got("d_scales", n)[:, q * P : (q + 1) * P],
+                    out=got("acc", b_tile)[:],
+                    lhsT=got("d_codes", n)[:, words].bitcast(E5M2_X4),
+                    lhsT_scale=got("d_scales", n)[:, words],
                     rhs=w_codes[:, q * HALVES + half, :].bitcast(E4M3_X4),
                     rhs_scale=w_scales[:, q * HALVES + half, :],
-                    start=(half == 0 and q == 0),
-                    stop=(half == HALVES - 1 and q == GATES - 1),
+                    start=(passes_done[b_tile] == 1),
+                    stop=(passes_done[b_tile] == GATES * HALVES),
                 )
-            if half == HALVES - 1:
-                result = work.tile([P, I_DIM], F32)
-                nc.scalar.copy(out=result[:], in_=acc[:])
-                nc.sync.dma_start(out=out[batch_rows(n), :], in_=result[:])
+
+        def store(b_tile):
+            result = work.tile([P, I_DIM], F32)
+            nc.scalar.copy(out=result[:], in_=got("acc", b_tile)[:])
+            nc.sync.dma_start(out=out[b_tile * P : (b_tile + 1) * P, :], in_=result[:])
 
         def run(step, n, count=GROUPS):
             if 0 <= n < count:
                 step(n)
 
+        multiplies_mid = {
+            4: [(n, (0, 1)) for n in (0, 1)],
+            5: [(n, (2,)) for n in range(2 * HALVES)],
+            6: [(4, tuple(SLOT))],
+            7: [(6, tuple(SLOT))],
+            8: [(7, tuple(SLOT))],
+        }
+        multiplies_end = {
+            4: [(n, (0, 1)) for n in (2, 3)],
+            5: [(n, (3,)) for n in range(2 * HALVES)],
+            6: [(5, tuple(SLOT))],
+        }
+        stores = {6: (0, 1), 7: (2,)}
+        last = GROUPS - 1
+        scalar_pieces = [(q, piece) for q in range(GATES) for piece in range(W_PIECES - 1)]
+        scalar_pieces_of_round = {0: (0, 2), 1: (2, 5), 2: (5, 8), 3: (8, 11), 4: (11, 12)}
+
         for j in range(-3, GROUPS + 1):
             run(load_group, j + 3)
-            run(load_weight, j + 2, GATES)
-            if 0 <= j < GATES:
-                for piece in range(W_PIECES - 1):
-                    regroup_weight(nc.scalar.copy, j, piece)
-            run(tanh_of("tf", "zf", -0.5), j + 2)
-            run(tanh_of("ti", "zi", -0.5), j + 2)
-            run(tanh_of("g", "zg", 1.0), j + 2)
-
-            run(quantise_dgates, j - 1)
-            run(op_m1, j + 1)
-            run(op_tf_m1, j + 1)
-            run(op_m2, j + 1)
-            run(turn_sum("s", "m1", "m2"), j + 1)
-            run(act_tc, j + 1)
+            run(load_weight, j + 1, GATES)
+            for b_tile in stores.get(j, ()):
+                store(b_tile)
 
             run(op_e, j)
-            run(turn_sum("pf", "tf_m1", "m1"), j)
-            run(op_d_o, j)
-            run(turn_sum("ti", "ti"), j)
+            run(turn_sum("pf", "pf"), j)
+            run(op_d_o, j - 1, last)
+            run(turn_sum("q", "q"), j)
             run(op_d_cy, j)
-            run(turn_gcy, j + 1)
-            run(tanh_of("to", "zo", -0.5), j + 2)
-            run(act_half_g2, j + 2)
+            run(turn_sum("gib", "g", "m2"), j)
 
+            run(quantise_dgates, j - 1, last)
+            if 0 <= j - 1 < GATES:
+                regroup_weight(nc.vector.tensor_copy, j - 1, W_PIECES - 1)
+            run(op_m2, j + 1)
+            run(op_m1, j + 1)
+            for pair in multiplies_mid.get(j, ()):
+                multiply(*pair)
+            run(turn_sum("s", "m2", "m1"), j + 1)
+            run(quantise_weight, j - 2, GATES)
             run(op_hn, j + 1)
-            run(op_to_hn, j + 1)
-            run(op_pi, j + 1)
-            if 0 <= j < GATES:
-                regroup_weight(nc.vector.tensor_copy, j, W_PIECES - 1)
+            run(op_q, j + 1)
+            run(op_pf, j + 1)
+            run(act_tc, j + 1)
 
-            run(op_eg, j)
-            run(turn_sum("half_g2", "half_g2"), j + 1)
-            run(op_d_i, j)
-            run(turn_sum("pi", "pi"), j + 1)
+            run(op_i_d, j)
+            run(turn_sum("ib", "ib"), j + 1)
+            if j == last:
+                op_d_o(j)
             run(op_d_f, j)
             run(turn_sum("hn", "hn"), j + 1)
+            run(op_d_i, j)
+            run(turn_gcy, j + 1)
+            if j == last:
+                quantise_dgates(j, 0, 2)
             run(op_d_g, j)
-            run(turn_sum("q", "to_hn", "hn"), j + 1)
+            run(turn_sum("g2", "g2"), j + 1)
+            if j == last:
+                quantise_dgates(j, 2, 3)
+                quantise_dgates(j, 3, 4)
+            for pair in multiplies_end.get(j, ()):
+                multiply(*pair)
 
-            run(quantise_weight, j - 1, GATES)
-            if j >= GATES:
-                for n in range(0 if j == GATES else j - 1, j):
-                    multiply(n)
+            run(act("ib", "zi", SIGMOID, -1.0), j + 2)
+            run(act("g", "zg", TANH), j + 2)
+            run(act("fb", "zf", SIGMOID, -1.0), j + 2)
+            run(act("ob", "zo", SIGMOID, -1.0), j + 2)
+            run(act("g2", "g", SQUARE), j + 2)
+            for i in range(*scalar_pieces_of_round.get(j, (0,))):
+                regroup_weight(nc.scalar.copy, *scalar_pieces[i])
+        store(B // P - 1)

@@ -25,6 +25,7 @@ SLOT = {GATE_O: 0, GATE_F: 1, GATE_I: 2, GATE_G: 3}
 HALVES = H // K_PASS
 GROUPS = (B // P) * HALVES
 W_PIECES = 4
+PASSES_AT_ONCE = 2
 W_PIECE_COLS = HALVES * I_DIM // W_PIECES
 
 FLOPS = 2 * B * GATES * H * I_DIM
@@ -191,73 +192,78 @@ def tile_ta_lstmcell_v_kernel(
             )
 
         passes_done = {}
+        passes_due = []
+        to_store = []
 
-        def multiply(n, gate_list=tuple(SLOT)):
+        def multiply(n, q):
             b_tile, half = divmod(n, HALVES)
             if b_tile not in passes_done:
                 new(psum, "acc", b_tile, F32, (P, I_DIM), bufs=2)
                 passes_done[b_tile] = 0
-            for q in gate_list:
-                passes_done[b_tile] += 1
-                words = slice(SLOT[q] * P, (SLOT[q] + 1) * P)
-                nc.tensor.matmul_mx(
-                    out=got("acc", b_tile)[:],
-                    lhsT=got("d_codes", n)[:, words].bitcast(E5M2_X4),
-                    lhsT_scale=got("d_scales", n)[:, words],
-                    rhs=w_codes[:, q * HALVES + half, :].bitcast(E4M3_X4),
-                    rhs_scale=w_scales[:, q * HALVES + half, :],
-                    start=(passes_done[b_tile] == 1),
-                    stop=(passes_done[b_tile] == GATES * HALVES),
-                )
+            passes_done[b_tile] += 1
+            words = slice(SLOT[q] * P, (SLOT[q] + 1) * P)
+            nc.tensor.matmul_mx(
+                out=got("acc", b_tile)[:],
+                lhsT=got("d_codes", n)[:, words].bitcast(E5M2_X4),
+                lhsT_scale=got("d_scales", n)[:, words],
+                rhs=w_codes[:, q * HALVES + half, :].bitcast(E4M3_X4),
+                rhs_scale=w_scales[:, q * HALVES + half, :],
+                start=(passes_done[b_tile] == 1),
+                stop=(passes_done[b_tile] == GATES * HALVES),
+            )
+            if passes_done[b_tile] == GATES * HALVES:
+                to_store.extend([b_tile])
 
-        def store(b_tile):
-            result = work.tile([P, I_DIM], F32)
-            nc.scalar.copy(out=result[:], in_=got("acc", b_tile)[:])
-            nc.sync.dma_start(out=out[b_tile * P : (b_tile + 1) * P, :], in_=result[:])
+        def multiply_due():
+            for i in range(min(PASSES_AT_ONCE, len(passes_due))):
+                multiply(*passes_due[0])
+                passes_due.remove(passes_due[0])
+
+        def store_finished():
+            for b_tile in to_store:
+                result = work.tile([P, I_DIM], F32)
+                nc.scalar.copy(out=result[:], in_=got("acc", b_tile)[:])
+                nc.sync.dma_start(out=out[b_tile * P : (b_tile + 1) * P, :], in_=result[:])
+            to_store.clear()
 
         def run(step, n, count=GROUPS):
             if 0 <= n < count:
                 step(n)
 
-        multiplies_mid = {
-            4: [(n, (0, 1)) for n in (0, 1)],
-            5: [(n, (2,)) for n in range(2 * HALVES)],
-            6: [(4, tuple(SLOT))],
-            7: [(6, tuple(SLOT))],
-            8: [(7, tuple(SLOT))],
+        due = {
+            2: [(0, 0), (1, 0)],
+            3: [(2, 0), (0, 1), (1, 1), (2, 1)],
+            4: [(3, 0), (3, 1)] + [(n, 2) for n in range(4)],
+            5: [(n, 3) for n in range(4)],
+            6: [(4, q) for q in SLOT] + [(5, q) for q in SLOT],
+            7: [(6, q) for q in SLOT] + [(7, q) for q in SLOT],
         }
-        multiplies_end = {
-            4: [(n, (0, 1)) for n in (2, 3)],
-            5: [(n, (3,)) for n in range(2 * HALVES)],
-            6: [(5, tuple(SLOT))],
-        }
-        stores = {6: (0, 1), 7: (2,)}
         last = GROUPS - 1
         scalar_pieces = [(q, piece) for q in range(GATES) for piece in range(W_PIECES - 1)]
         scalar_pieces_of_round = {0: (0, 2), 1: (2, 5), 2: (5, 8), 3: (8, 11), 4: (11, 12)}
 
-        for j in range(-3, GROUPS + 1):
+        for j in range(-3, GROUPS):
             run(load_group, j + 3)
             run(load_weight, j + 1, GATES)
-            for b_tile in stores.get(j, ()):
-                store(b_tile)
 
             run(op_e, j)
             run(turn_sum("pf", "pf"), j)
             run(op_d_o, j - 1, last)
             run(turn_sum("q", "q"), j)
+            multiply_due()
             run(op_d_cy, j)
             run(turn_sum("gib", "g", "m2"), j)
 
+            run(op_m2, j + 1)
+            run(op_m1, j + 1)
+            run(turn_sum("s", "m2", "m1"), j + 1)
+            multiply_due()
             run(quantise_dgates, j - 1, last)
             if 0 <= j - 1 < GATES:
                 regroup_weight(nc.vector.tensor_copy, j - 1, W_PIECES - 1)
-            run(op_m2, j + 1)
-            run(op_m1, j + 1)
-            for pair in multiplies_mid.get(j, ()):
-                multiply(*pair)
-            run(turn_sum("s", "m2", "m1"), j + 1)
             run(quantise_weight, j - 2, GATES)
+            passes_due.extend(due.get(j, ()))
+            multiply_due()
             run(op_hn, j + 1)
             run(op_q, j + 1)
             run(op_pf, j + 1)
@@ -275,11 +281,13 @@ def tile_ta_lstmcell_v_kernel(
                 quantise_dgates(j, 0, 2)
             run(op_d_g, j)
             run(turn_sum("g2", "g2"), j + 1)
+            if j < last:
+                multiply_due()
             if j == last:
                 quantise_dgates(j, 2, 3)
                 quantise_dgates(j, 3, 4)
-            for pair in multiplies_end.get(j, ()):
-                multiply(*pair)
+                for n, q in passes_due:
+                    multiply(n, q)
 
             run(act("ib", "zi", SIGMOID, -1.0), j + 2)
             run(act("g", "zg", TANH), j + 2)
@@ -288,4 +296,4 @@ def tile_ta_lstmcell_v_kernel(
             run(act("g2", "g", SQUARE), j + 2)
             for i in range(*scalar_pieces_of_round.get(j, (0,))):
                 regroup_weight(nc.scalar.copy, *scalar_pieces[i])
-        store(B // P - 1)
+            store_finished()

@@ -21,11 +21,12 @@ PACK = 4
 K_PASS = P * PACK
 GATES = 4
 GATE_I, GATE_F, GATE_G, GATE_O = 0, 1, 2, 3
-SLOT = {GATE_O: 0, GATE_F: 1, GATE_I: 2, GATE_G: 3}
+SLOT = {GATE_F: 0, GATE_O: 1, GATE_I: 2, GATE_G: 3}
 HALVES = H // K_PASS
 GROUPS = (B // P) * HALVES
 W_PIECES = 4
 PASSES_AT_ONCE = 2
+HEAD_WARM = 9
 W_PIECE_COLS = HALVES * I_DIM // W_PIECES
 
 FLOPS = 2 * B * GATES * H * I_DIM
@@ -68,8 +69,8 @@ def tile_ta_lstmcell_v_kernel(
         def got(name, n):
             return tiles[(name, n)]
 
-        def packed(name, n):
-            return got(name, n)[:].rearrange("p (b t) -> p b t", t=PACK)
+        def packed(name, n, rows=slice(0, P)):
+            return got(name, n)[:, rows.start * PACK : rows.stop * PACK].rearrange("p (b t) -> p b t", t=PACK)
 
         def bank(name, n):
             return got(name + "_t", n)[:].rearrange("p (t b) -> p b t", t=PACK)
@@ -78,18 +79,23 @@ def tile_ta_lstmcell_v_kernel(
             for name, start in (("zi", GATE_I * H), ("zg", GATE_G * H), ("zf", GATE_F * H), ("ca", None), ("zo", GATE_O * H)):
                 src = cx_adj[batch_rows(n), hidden_cols(n)] if start is None else gates[batch_rows(n), hidden_cols(n, start)]
                 nc.sync.dma_start(out=new(raw, name, n)[:], in_=src)
-            nc.sync.dma_start(
-                out=new(raw, "grads", n, BF16, (P, 2, K_PASS))[:],
-                in_=grad_out[:, batch_rows(n), hidden_cols(n)].rearrange("s b h -> b s h"),
-            )
+            for s, name in enumerate(("g_hy", "g_cy")):
+                nc.sync.dma_start(out=new(raw, name, n, BF16)[:], in_=grad_out[s, batch_rows(n), hidden_cols(n)])
 
-        def load_weight(q):
+        def load_weight(q, c):
+            if c == 0:
+                new(const, "w_raw%d" % q, q, BF16, (P, HALVES, PACK, I_DIM))
+            first = q * H + c * K_PASS
             nc.sync.dma_start(
-                out=new(const, "w_raw%d" % q, q, BF16, (P, HALVES, PACK, I_DIM))[:],
-                in_=weight_ih[q * H : (q + 1) * H, :].rearrange("(c t p) n -> p c t n", t=PACK, p=P),
+                out=got("w_raw%d" % q, q)[:, c, :, :],
+                in_=weight_ih[first : first + K_PASS, :].rearrange("(t p) n -> p t n", p=P),
             )
 
         bank_of = {"s": "s", "hn": "hn_pf", "pf": "hn_pf", "q": "q", "ib": "ib", "gcy": "gcy_gib", "gib": "gcy_gib", "g2": "g2"}
+
+        def warm(bank_tile, count):
+            for i in range(count):
+                nc.tensor.matmul(out=bank_tile[:, :P], lhsT=ident_f32[:], rhs=ident_f32[:], start=True, stop=True)
 
         def turn(name, n, terms):
             turned = new(psum, name + "_t", n, terms[0].dtype, tag=bank_of[name])
@@ -106,15 +112,24 @@ def tile_ta_lstmcell_v_kernel(
             return lambda n: turn(name, n, [got(term, n) for term in term_names])
 
         def turn_gcy(n):
-            turn("gcy", n, [got("grads", n)[:, 1, :]])
+            turned = new(psum, "gcy_t", n, tag=bank_of["gcy"])
+            for t in range(PACK):
+                block = slice(t * P, (t + 1) * P)
+                nc.tensor.matmul(out=turned[:, block], lhsT=got("g_cy", n)[:, block], rhs=ident_bf16[:], start=True, stop=True)
+
+        def row_parts(n):
+            return (slice(0, P // 2), slice(P // 2, P)) if n == 0 else (slice(0, P),)
 
         def act(name, src, func, scale=1.0):
             return lambda n: nc.scalar.activation(out=new(acts, name, n)[:], in_=got(src, n)[:], func=func, scale=scale)
 
         def act_tc(n):
             new(work, "tc", n)
-            nc.scalar.activation(out=packed("tc", n), in_=bank("s", n), func=TANH, scale=-1.0)
-            nc.scalar.activation(out=new(work, "tc2", n)[:], in_=got("tc", n)[:], func=SQUARE)
+            new(work, "tc2", n)
+            for rows in row_parts(n):
+                nc.scalar.activation(out=packed("tc", n, rows), in_=bank("s", n)[:, rows, :], func=TANH, scale=-1.0)
+            for rows in row_parts(n):
+                nc.scalar.activation(out=packed("tc2", n, rows), in_=packed("tc", n, rows), func=SQUARE)
 
         def stt(out, in0, scalar, in1, op0, op1=MULT):
             nc.vector.scalar_tensor_tensor(out=out, in0=in0, scalar=scalar, in1=in1, op0=op0, op1=op1)
@@ -126,7 +141,7 @@ def tile_ta_lstmcell_v_kernel(
             stt(new(work, "m2", n)[:], got("ib", n)[:], -1.0, got("g", n)[:], ADD)
 
         def op_hn(n):
-            stt(new(work, "hn", n)[:], got("ob", n)[:], -1.0, got("grads", n)[:, 0, :], ADD)
+            stt(new(work, "hn", n)[:], got("ob", n)[:], -1.0, got("g_hy", n)[:], ADD)
 
         def op_pf(n):
             nc.gpsimd.tensor_tensor(out=new(work, "pf", n)[:], in0=got("fb", n)[:], in1=got("m1", n)[:], op=MULT)
@@ -139,7 +154,8 @@ def tile_ta_lstmcell_v_kernel(
 
         def op_e(n):
             new(work, "e", n)
-            stt(packed("e", n), packed("tc2", n), -1.0, bank("hn", n), ADD)
+            for rows in row_parts(n):
+                stt(packed("e", n, rows), packed("tc2", n, rows), -1.0, bank("hn", n)[:, rows, :], ADD)
 
         def op_d_o(n):
             stt(dgate(n, GATE_O), bank("q", n), -1.0, packed("tc", n), MULT)
@@ -149,11 +165,11 @@ def tile_ta_lstmcell_v_kernel(
             nc.vector.tensor_tensor(out=packed("d_cy", n), in0=packed("e", n), in1=bank("gcy", n), op=ADD)
 
         def op_i_d(n):
-            new(work, "dq", n, BF16, (P, GATES, K_PASS), align_bytes=64)
             new(work, "i_d", n)
             stt(packed("i_d", n), bank("ib", n), -1.0, packed("d_cy", n), ADD)
 
         def op_d_f(n):
+            new(work, "dq", n, BF16, (P, GATES, K_PASS), align_bytes=64)
             stt(dgate(n, GATE_F), bank("pf", n), -1.0, packed("d_cy", n), MULT)
 
         def op_d_i(n):
@@ -182,6 +198,9 @@ def tile_ta_lstmcell_v_kernel(
                 .rearrange("p (m i) t -> p m t i", i=4),
                 in_=got("w_raw%d" % q, q)[:, c, :, part : part + W_PIECE_COLS].rearrange("p t (m i) -> p m t i", i=4),
             )
+
+        def gpsimd_copy(out, in_):
+            nc.gpsimd.tensor_scalar(out=out, in0=in_, scalar1=1.0, scalar2=0.0, op0=MULT, op1=ADD)
 
         def quantise_weight(q):
             passes = slice(q * HALVES, (q + 1) * HALVES)
@@ -239,51 +258,65 @@ def tile_ta_lstmcell_v_kernel(
             7: [(6, q) for q in SLOT] + [(7, q) for q in SLOT],
         }
         last = GROUPS - 1
-        scalar_pieces = [(q, piece) for q in range(GATES) for piece in range(W_PIECES - 1)]
-        scalar_pieces_of_round = {0: (0, 2), 1: (2, 5), 2: (5, 8), 3: (8, 11), 4: (11, 12)}
+        vector_pieces = {0: [(0, 0), (0, 1)]}
+        gpsimd_pieces = {2: [(1, 3)], 3: [(2, 3)], 4: [(3, 3)]}
+        scalar_pieces = {
+            0: [(0, 2), (0, 3)],
+            1: [(1, 0), (1, 1), (1, 2)],
+            2: [(2, 0), (2, 1), (2, 2)],
+            3: [(3, 0), (3, 1), (3, 2)],
+        }
 
+        warm(new(psum, "head", 0, tag=bank_of["s"]), HEAD_WARM)
         for j in range(-3, GROUPS):
             run(load_group, j + 3)
-            run(load_weight, j + 1, GATES)
+            if j == -3:
+                load_weight(0, 0)
+            if j == -2:
+                load_weight(0, 1)
+            if 0 < j + 1 < GATES:
+                for c in range(HALVES):
+                    load_weight(j + 1, c)
 
             run(op_e, j)
             run(turn_sum("pf", "pf"), j)
-            run(op_d_o, j - 1, last)
-            run(turn_sum("q", "q"), j)
-            multiply_due()
+            run(op_d_g, j - 1, last)
+            run(turn_sum("g2", "g2"), j)
+            if j < last:
+                multiply_due()
             run(op_d_cy, j)
             run(turn_sum("gib", "g", "m2"), j)
+            run(turn_sum("q", "q"), j)
 
             run(op_m2, j + 1)
             run(op_m1, j + 1)
             run(turn_sum("s", "m2", "m1"), j + 1)
             multiply_due()
             run(quantise_dgates, j - 1, last)
-            if 0 <= j - 1 < GATES:
-                regroup_weight(nc.vector.tensor_copy, j - 1, W_PIECES - 1)
+            for q, piece in vector_pieces.get(j, ()):
+                regroup_weight(nc.vector.tensor_copy, q, piece)
             run(quantise_weight, j - 2, GATES)
             passes_due.extend(due.get(j, ()))
             multiply_due()
             run(op_hn, j + 1)
-            run(op_q, j + 1)
             run(op_pf, j + 1)
+            run(op_q, j + 1)
+            for q, piece in gpsimd_pieces.get(j, ()):
+                regroup_weight(gpsimd_copy, q, piece)
             run(act_tc, j + 1)
 
-            run(op_i_d, j)
-            run(turn_sum("ib", "ib"), j + 1)
-            if j == last:
-                op_d_o(j)
             run(op_d_f, j)
             run(turn_sum("hn", "hn"), j + 1)
+            run(op_i_d, j)
+            run(turn_sum("ib", "ib"), j + 1)
+            run(op_d_o, j)
             run(op_d_i, j)
             run(turn_gcy, j + 1)
-            if j == last:
-                quantise_dgates(j, 0, 2)
-            run(op_d_g, j)
-            run(turn_sum("g2", "g2"), j + 1)
             if j < last:
                 multiply_due()
-            if j == last:
+            else:
+                quantise_dgates(j, 0, 2)
+                op_d_g(j)
                 quantise_dgates(j, 2, 3)
                 quantise_dgates(j, 3, 4)
                 for n, q in passes_due:
@@ -294,6 +327,6 @@ def tile_ta_lstmcell_v_kernel(
             run(act("fb", "zf", SIGMOID, -1.0), j + 2)
             run(act("ob", "zo", SIGMOID, -1.0), j + 2)
             run(act("g2", "g", SQUARE), j + 2)
-            for i in range(*scalar_pieces_of_round.get(j, (0,))):
-                regroup_weight(nc.scalar.copy, *scalar_pieces[i])
+            for q, piece in scalar_pieces.get(j, ()):
+                regroup_weight(nc.scalar.copy, q, piece)
             store_finished()

@@ -118,7 +118,7 @@ def tile_ta_lstmcell_v_kernel(
                 nc.tensor.matmul(out=turned[:, block], lhsT=got("g_cy", n)[:, block], rhs=ident_bf16[:], start=True, stop=True)
 
         def row_parts(n):
-            return (slice(0, P // 2), slice(P // 2, P)) if n == 0 else (slice(0, P),)
+            return (slice(0, P // 2), slice(P // 2, P)) if n >= 0 else (slice(0, P),)
 
         def act(name, src, func, scale=1.0):
             return lambda n: nc.scalar.activation(out=new(acts, name, n)[:], in_=got(src, n)[:], func=func, scale=scale)
@@ -135,7 +135,9 @@ def tile_ta_lstmcell_v_kernel(
             nc.vector.scalar_tensor_tensor(out=out, in0=in0, scalar=scalar, in1=in1, op0=op0, op1=op1)
 
         def op_m1(n):
-            stt(new(work, "m1", n)[:], got("fb", n)[:], -1.0, got("ca", n)[:], ADD)
+            new(work, "m1", n)
+            for cols in (slice(0, K_PASS // 2), slice(K_PASS // 2, K_PASS)):
+                stt(got("m1", n)[:, cols], got("fb", n)[:, cols], -1.0, got("ca", n)[:, cols], ADD)
 
         def op_m2(n):
             stt(new(work, "m2", n)[:], got("ib", n)[:], -1.0, got("g", n)[:], ADD)

@@ -27,6 +27,7 @@ GROUPS = (B // P) * HALVES
 W_PIECES = 4
 PASSES_AT_ONCE = 2
 HEAD_WARM = 9
+R_FROM = 6
 W_PIECE_COLS = HALVES * I_DIM // W_PIECES
 
 FLOPS = 2 * B * GATES * H * I_DIM
@@ -91,7 +92,7 @@ def tile_ta_lstmcell_v_kernel(
                 in_=weight_ih[first : first + K_PASS, :].rearrange("(t p) n -> p t n", p=P),
             )
 
-        bank_of = {"s": "s", "hn": "hn_pf", "pf": "hn_pf", "q": "q", "ib": "ib", "gcy": "gcy_gib", "gib": "gcy_gib", "g2": "g2"}
+        bank_of = {"s": "s", "hn": "hn_pf", "pf": "hn_pf", "q": "q", "ib": "ib", "gcy": "gcy_gib", "gib": "gcy_gib", "pi": "gcy_gib", "g2": "g2", "r": "g2"}
 
         def warm(bank_tile, count):
             for i in range(count):
@@ -110,6 +111,25 @@ def tile_ta_lstmcell_v_kernel(
 
         def turn_sum(name, *term_names):
             return lambda n: turn(name, n, [got(term, n) for term in term_names])
+
+        def short(n):
+            return n >= R_FROM
+
+        def turn_gib(n):
+            if short(n):
+                turn("pi", n, [got("pi", n)])
+            else:
+                turn("gib", n, [got("g", n), got("m2", n)])
+
+        def turn_g2(n):
+            if short(n):
+                turn("r", n, [got("r", n)])
+            else:
+                turn("g2", n, [got("g2", n)])
+
+        def turn_ib(n):
+            if not short(n):
+                turn("ib", n, [got("ib", n)])
 
         def turn_gcy(n):
             turned = new(psum, "gcy_t", n, tag=bank_of["gcy"])
@@ -145,6 +165,12 @@ def tile_ta_lstmcell_v_kernel(
         def op_hn(n):
             stt(new(work, "hn", n)[:], got("ob", n)[:], -1.0, got("g_hy", n)[:], ADD)
 
+        def op_r(n):
+            stt(new(work, "r", n)[:], got("g2", n)[:], -1.0, got("i", n)[:], ADD)
+
+        def op_pi(n):
+            nc.gpsimd.tensor_tensor(out=new(work, "pi", n)[:], in0=got("ib", n)[:], in1=got("m2", n)[:], op=MULT)
+
         def op_pf(n):
             nc.gpsimd.tensor_tensor(out=new(work, "pf", n)[:], in0=got("fb", n)[:], in1=got("m1", n)[:], op=MULT)
 
@@ -167,6 +193,8 @@ def tile_ta_lstmcell_v_kernel(
             nc.vector.tensor_tensor(out=packed("d_cy", n), in0=packed("e", n), in1=bank("gcy", n), op=ADD)
 
         def op_i_d(n):
+            if short(n):
+                return
             new(work, "i_d", n)
             stt(packed("i_d", n), bank("ib", n), -1.0, packed("d_cy", n), ADD)
 
@@ -175,10 +203,16 @@ def tile_ta_lstmcell_v_kernel(
             stt(dgate(n, GATE_F), bank("pf", n), -1.0, packed("d_cy", n), MULT)
 
         def op_d_i(n):
-            stt(dgate(n, GATE_I), bank("gib", n), -1.0, packed("i_d", n), MULT)
+            if short(n):
+                stt(dgate(n, GATE_I), bank("pi", n), -1.0, packed("d_cy", n), MULT)
+            else:
+                stt(dgate(n, GATE_I), bank("gib", n), -1.0, packed("i_d", n), MULT)
 
         def op_d_g(n):
-            stt(dgate(n, GATE_G), bank("g2", n), -1.0, packed("i_d", n), ADD)
+            if short(n):
+                stt(dgate(n, GATE_G), bank("r", n), -1.0, packed("d_cy", n), MULT)
+            else:
+                stt(dgate(n, GATE_G), bank("g2", n), -1.0, packed("i_d", n), ADD)
 
         def quantise_dgates(n, first=0, last=GATES):
             if first == 0:
@@ -283,12 +317,12 @@ def tile_ta_lstmcell_v_kernel(
             run(op_e, j)
             run(turn_sum("pf", "pf"), j)
             run(op_d_g, j - 1, last)
-            run(turn_sum("g2", "g2"), j)
+            run(turn_g2, j)
             if j < last:
                 multiply_due()
-            run(op_d_cy, j)
-            run(turn_sum("gib", "g", "m2"), j)
             run(turn_sum("q", "q"), j)
+            run(op_d_cy, j)
+            run(turn_gib, j)
 
             run(op_m2, j + 1)
             run(op_m1, j + 1)
@@ -301,8 +335,12 @@ def tile_ta_lstmcell_v_kernel(
             passes_due.extend(due.get(j, ()))
             multiply_due()
             run(op_hn, j + 1)
+            if short(j + 1):
+                run(op_r, j + 1)
             run(op_pf, j + 1)
             run(op_q, j + 1)
+            if short(j + 1):
+                run(op_pi, j + 1)
             for q, piece in gpsimd_pieces.get(j, ()):
                 regroup_weight(gpsimd_copy, q, piece)
             run(act_tc, j + 1)
@@ -310,7 +348,7 @@ def tile_ta_lstmcell_v_kernel(
             run(op_d_f, j)
             run(turn_sum("hn", "hn"), j + 1)
             run(op_i_d, j)
-            run(turn_sum("ib", "ib"), j + 1)
+            run(turn_ib, j + 1)
             run(op_d_o, j)
             run(op_d_i, j)
             run(turn_gcy, j + 1)
@@ -329,6 +367,8 @@ def tile_ta_lstmcell_v_kernel(
             run(act("fb", "zf", SIGMOID, -1.0), j + 2)
             run(act("ob", "zo", SIGMOID, -1.0), j + 2)
             run(act("g2", "g", SQUARE), j + 2)
+            if short(j + 2):
+                run(act("i", "zi", SIGMOID), j + 2)
             for q, piece in scalar_pieces.get(j, ()):
                 regroup_weight(nc.scalar.copy, q, piece)
             store_finished()

@@ -277,8 +277,11 @@ def tile_ta_lstmcell_v_kernel(
         def store_finished():
             for b_tile in to_store:
                 result = work.tile([P, I_DIM], F32)
-                nc.scalar.copy(out=result[:], in_=got("acc", b_tile)[:])
-                nc.sync.dma_start(out=out[b_tile * P : (b_tile + 1) * P, :], in_=result[:])
+                halves = 2 if b_tile == B // P - 1 else 1
+                for i in range(halves):
+                    cols = slice(i * I_DIM // halves, (i + 1) * I_DIM // halves)
+                    nc.scalar.copy(out=result[:, cols], in_=got("acc", b_tile)[:, cols])
+                    nc.sync.dma_start(out=out[b_tile * P : (b_tile + 1) * P, cols], in_=result[:, cols])
             to_store.clear()
 
         def run(step, n, count=GROUPS):
@@ -289,15 +292,15 @@ def tile_ta_lstmcell_v_kernel(
             2: [(0, 0), (1, 0)],
             3: [(2, 0), (0, 1), (1, 1), (2, 1)],
             4: [(3, 0), (3, 1)] + [(n, 2) for n in range(4)],
-            5: [(n, 3) for n in range(4)],
-            6: [(4, q) for q in SLOT] + [(5, q) for q in SLOT],
+            5: [(n, 3) for n in range(4)] + [(4, GATE_F), (4, GATE_O)],
+            6: [(4, GATE_I), (4, GATE_G)] + [(5, q) for q in SLOT],
             7: [(6, q) for q in SLOT] + [(7, q) for q in SLOT],
         }
         last = GROUPS - 1
-        vector_pieces = {0: [(0, 0), (0, 1)]}
-        gpsimd_pieces = {2: [(1, 3)], 3: [(2, 3)], 4: [(3, 3)]}
+        vector_pieces = {0: [(0, 0)]}
+        gpsimd_pieces = {0: [(0, 1)], 1: [(0, 3)], 2: [(1, 3)], 3: [(2, 3)], 4: [(3, 3)]}
         scalar_pieces = {
-            0: [(0, 2), (0, 3)],
+            0: [(0, 2)],
             1: [(1, 0), (1, 1), (1, 2)],
             2: [(2, 0), (2, 1), (2, 2)],
             3: [(3, 0), (3, 1), (3, 2)],
@@ -354,6 +357,8 @@ def tile_ta_lstmcell_v_kernel(
             run(turn_gcy, j + 1)
             if j < last:
                 multiply_due()
+                if j == 5:
+                    multiply_due()
             else:
                 quantise_dgates(j, 0, 2)
                 op_d_g(j)

@@ -24,6 +24,7 @@ GATE_I, GATE_F, GATE_G, GATE_O = 0, 1, 2, 3
 SLOT = {GATE_F: 0, GATE_O: 1, GATE_I: 2, GATE_G: 3}
 HALVES = H // K_PASS
 GROUPS = (B // P) * HALVES
+RUN = 8
 W_PIECES = 4
 PASSES_AT_ONCE = 2
 HEAD_WARM = 9
@@ -231,8 +232,8 @@ def tile_ta_lstmcell_v_kernel(
             c, part = divmod(piece * W_PIECE_COLS, I_DIM)
             copy(
                 out=got("w_grouped", q)[:, piece * W_PIECE_COLS : (piece + 1) * W_PIECE_COLS, :]
-                .rearrange("p (m i) t -> p m t i", i=4),
-                in_=got("w_raw%d" % q, q)[:, c, :, part : part + W_PIECE_COLS].rearrange("p t (m i) -> p m t i", i=4),
+                .rearrange("p (m i) t -> p m t i", i=RUN),
+                in_=got("w_raw%d" % q, q)[:, c, :, part : part + W_PIECE_COLS].rearrange("p t (m i) -> p m t i", i=RUN),
             )
 
         def gpsimd_copy(out, in_):

@@ -114,7 +114,7 @@ def tile_ta_lstmcell_v_kernel(
             return lambda n: turn(name, n, [got(term, n) for term in term_names])
 
         def short(n):
-            return n >= R_FROM
+            return n in (0, 6, 7)
 
         def turn_gib(n):
             if short(n):
@@ -157,8 +157,7 @@ def tile_ta_lstmcell_v_kernel(
 
         def op_m1(n):
             new(work, "m1", n)
-            for cols in (slice(0, K_PASS // 2), slice(K_PASS // 2, K_PASS)):
-                stt(got("m1", n)[:, cols], got("fb", n)[:, cols], -1.0, got("ca", n)[:, cols], ADD)
+            stt(got("m1", n)[:], got("fb", n)[:], -1.0, got("ca", n)[:], ADD)
 
         def op_m2(n):
             stt(new(work, "m2", n)[:], got("ib", n)[:], -1.0, got("g", n)[:], ADD)

from contextlib import ExitStack

import concourse.mybir as mybir
from concourse.masks import make_identity

F32 = mybir.dt.float32
BF16 = mybir.dt.bfloat16
U32 = mybir.dt.uint32
U8 = mybir.dt.uint8
E4M3_X4 = mybir.dt.float8_e4m3fn_x4
E5M2_X4 = mybir.dt.float8_e5m2_x4
ADD = mybir.AluOpType.add
MULT = mybir.AluOpType.mult
TANH = mybir.ActivationFunctionType.Tanh
SIGMOID = mybir.ActivationFunctionType.Sigmoid
SQUARE = mybir.ActivationFunctionType.Square

B, I_DIM, H = 512, 512, 1024
P = 128
PACK = 4
K_PASS = P * PACK
GATES = 4
GATE_I, GATE_F, GATE_G, GATE_O = 0, 1, 2, 3
SLOT = {GATE_F: 0, GATE_O: 1, GATE_I: 2, GATE_G: 3}
HALVES = H // K_PASS
GROUPS = (B // P) * HALVES
RUN = 8
W_PIECES = 4
PASSES_AT_ONCE = 2
HEAD_WARM = 9
R_FROM = 6
W_PIECE_COLS = HALVES * I_DIM // W_PIECES

FLOPS = 2 * B * GATES * H * I_DIM
BYTES = 4 * B * GATES * H + 4 * B * H + 2 * 2 * B * H + 2 * GATES * H * I_DIM + 4 * B * I_DIM


def tile_ta_lstmcell_v_kernel(
    tc, x_in, t_in, hx, cx, weight_ih, weight_hh, bias_ih, bias_hh, w_decomp, b_decomp,
    gates, cx_adj, grad_out, out,
):
    nc = tc.nc
    tiles = {}

    with ExitStack() as stack:
        const = stack.enter_context(tc.tile_pool(name="const", bufs=1))
        raw = stack.enter_context(tc.tile_pool(name="raw", bufs=3))
        acts = stack.enter_context(tc.tile_pool(name="acts", bufs=3))
        work = stack.enter_context(tc.tile_pool(name="work", bufs=2))
        codes = stack.enter_context(tc.tile_pool(name="codes", bufs=GROUPS))
        psum = stack.enter_context(tc.psum_pool(name="psum", bufs=1))
        stack.enter_context(tc.manual_schedule())

        ident_f32 = const.tile([P, P], F32)
        make_identity(nc, ident_f32[:])
        ident_bf16 = const.tile([P, P], BF16)
        make_identity(nc, ident_bf16[:])
        w_codes = const.tile([P, GATES * HALVES, I_DIM], U32, align_bytes=64)
        w_scales = const.tile([P, GATES * HALVES, I_DIM], U8, align_bytes=64)

        def batch_rows(n):
            return slice((n // HALVES) * P, (n // HALVES + 1) * P)

        def hidden_cols(n, start=0):
            return slice(start + (n % HALVES) * K_PASS, start + (n % HALVES + 1) * K_PASS)

        def new(pool, name, n, dtype=F32, shape=(P, K_PASS), tag=None, **kw):
            tiles[(name, n)] = pool.tile(list(shape), dtype, name=name, tag=tag or name, **kw)
            return tiles[(name, n)]

        def got(name, n):
            return tiles[(name, n)]

        def packed(name, n, rows=slice(0, P)):
            return got(name, n)[:, rows.start * PACK : rows.stop * PACK].rearrange("p (b t) -> p b t", t=PACK)

        def bank(name, n):
            return got(name + "_t", n)[:].rearrange("p (t b) -> p b t", t=PACK)

        def load_group(n):
            for name, start in (("zi", GATE_I * H), ("zg", GATE_G * H), ("zf", GATE_F * H), ("ca", None), ("zo", GATE_O * H)):
                src = cx_adj[batch_rows(n), hidden_cols(n)] if start is None else gates[batch_rows(n), hidden_cols(n, start)]
                nc.sync.dma_start(out=new(raw, name, n)[:], in_=src)
            for s, name in enumerate(("g_hy", "g_cy")):
                nc.sync.dma_start(out=new(raw, name, n, BF16)[:], in_=grad_out[s, batch_rows(n), hidden_cols(n)])

        def load_weight(q, c):
            if c == 0:
                new(const, "w_raw%d" % q, q, BF16, (P, HALVES, PACK, I_DIM))
            first = q * H + c * K_PASS
            nc.sync.dma_start(
                out=got("w_raw%d" % q, q)[:, c, :, :],
                in_=weight_ih[first : first + K_PASS, :].rearrange("(t p) n -> p t n", p=P),
            )

        bank_of = {"s": "s", "hn": "hn_pf", "pf": "hn_pf", "q": "q", "ib": "ib", "gcy": "gcy_gib", "gib": "gcy_gib", "pi": "gcy_gib", "g2": "g2", "r": "g2"}

        def warm(bank_tile, count):
            for i in range(count):
                nc.tensor.matmul(out=bank_tile[:, :P], lhsT=ident_f32[:], rhs=ident_f32[:], start=True, stop=True)

        def turn(name, n, terms):
            turned = new(psum, name + "_t", n, terms[0].dtype, tag=bank_of[name])
            ident = ident_f32 if terms[0].dtype == F32 else ident_bf16
            for t in range(PACK):
                block = slice(t * P, (t + 1) * P)
                for term in terms:
                    nc.tensor.matmul(
                        out=turned[:, block], lhsT=term[:, block], rhs=ident[:], is_transpose=True,
                        start=(term is terms[0]), stop=(term is terms[-1]),
                    )

        def turn_sum(name, *term_names):
            return lambda n: turn(name, n, [got(term, n) for term in term_names])

        def short(n):
            return n in (0, 6, 7)

        def turn_gib(n):
            if short(n):
                turn("pi", n, [got("pi", n)])
            else:
                turn("gib", n, [got("g", n), got("m2", n)])

        def turn_g2(n):
            if short(n):
                turn("r", n, [got("r", n)])
            else:
                turn("g2", n, [got("g2", n)])

        def turn_ib(n):
            if not short(n):
                turn("ib", n, [got("ib", n)])

        def turn_gcy(n):
            turned = new(psum, "gcy_t", n, tag=bank_of["gcy"])
            for t in range(PACK):
                block = slice(t * P, (t + 1) * P)
                nc.tensor.matmul(out=turned[:, block], lhsT=got("g_cy", n)[:, block], rhs=ident_bf16[:], start=True, stop=True)

        def row_parts(n):
            return (slice(0, P // 2), slice(P // 2, P)) if n >= 0 else (slice(0, P),)

        def act(name, src, func, scale=1.0):
            return lambda n: nc.scalar.activation(out=new(acts, name, n)[:], in_=got(src, n)[:], func=func, scale=scale)

        def act_tc(n):
            new(work, "tc", n)
            new(work, "tc2", n)
            for rows in row_parts(n):
                nc.scalar.activation(out=packed("tc", n, rows), in_=bank("s", n)[:, rows, :], func=TANH, scale=-1.0)
            for rows in row_parts(n):
                nc.scalar.activation(out=packed("tc2", n, rows), in_=packed("tc", n, rows), func=SQUARE)

        def stt(out, in0, scalar, in1, op0, op1=MULT):
            nc.vector.scalar_tensor_tensor(out=out, in0=in0, scalar=scalar, in1=in1, op0=op0, op1=op1)

        def op_m1(n):
            new(work, "m1", n)
            stt(got("m1", n)[:], got("fb", n)[:], -1.0, got("ca", n)[:], ADD)

        def op_m2(n):
            stt(new(work, "m2", n)[:], got("ib", n)[:], -1.0, got("g", n)[:], ADD)

        def op_hn(n):
            stt(new(work, "hn", n)[:], got("ob", n)[:], -1.0, got("g_hy", n)[:], ADD)

        def op_r(n):
            stt(new(work, "r", n)[:], got("g2", n)[:], -1.0, got("i", n)[:], ADD)

        def op_pi(n):
            nc.gpsimd.tensor_tensor(out=new(work, "pi", n)[:], in0=got("ib", n)[:], in1=got("m2", n)[:], op=MULT)

        def op_pf(n):
            nc.gpsimd.tensor_tensor(out=new(work, "pf", n)[:], in0=got("fb", n)[:], in1=got("m1", n)[:], op=MULT)

        def op_q(n):
            nc.gpsimd.tensor_tensor(out=new(work, "q", n)[:], in0=got("ob", n)[:], in1=got("hn", n)[:], op=MULT)

        def dgate(n, q):
            return got("dq", n)[:, SLOT[q], :].rearrange("p (b t) -> p b t", t=PACK)

        def op_e(n):
            new(work, "e", n)
            for rows in row_parts(n):
                stt(packed("e", n, rows), packed("tc2", n, rows), -1.0, bank("hn", n)[:, rows, :], ADD)

        def op_d_o(n):
            stt(dgate(n, GATE_O), bank("q", n), -1.0, packed("tc", n), MULT)

        def op_d_cy(n):
            new(work, "d_cy", n)
            nc.vector.tensor_tensor(out=packed("d_cy", n), in0=packed("e", n), in1=bank("gcy", n), op=ADD)

        def op_i_d(n):
            if short(n):
                return
            new(work, "i_d", n)
            stt(packed("i_d", n), bank("ib", n), -1.0, packed("d_cy", n), ADD)

        def op_d_f(n):
            new(work, "dq", n, BF16, (P, GATES, K_PASS), align_bytes=64)
            stt(dgate(n, GATE_F), bank("pf", n), -1.0, packed("d_cy", n), MULT)

        def op_d_i(n):
            if short(n):
                stt(dgate(n, GATE_I), bank("pi", n), -1.0, packed("d_cy", n), MULT)
            else:
                stt(dgate(n, GATE_I), bank("gib", n), -1.0, packed("i_d", n), MULT)

        def op_d_g(n):
            if short(n):
                stt(dgate(n, GATE_G), bank("r", n), -1.0, packed("d_cy", n), MULT)
            else:
                stt(dgate(n, GATE_G), bank("g2", n), -1.0, packed("i_d", n), ADD)

        def quantise_dgates(n, first=0, last=GATES):
            if first == 0:
                new(codes, "d_codes", n, U32, (P, GATES * P), align_bytes=64)
                new(codes, "d_scales", n, U8, (P, GATES * P), align_bytes=64)
            cols = slice(first * P, last * P)
            nc.vector.quantize_mx(
                out=got("d_codes", n)[:, cols].bitcast(E5M2_X4),
                scales=got("d_scales", n)[:, cols],
                in_=got("dq", n)[:, first:last, :].rearrange("p q c -> p (q c)"),
            )

        def regroup_weight(copy, q, piece):
            if piece == 0:
                new(work, "w_grouped", q, BF16, (P, HALVES * I_DIM, PACK), align_bytes=64)
            c, part = divmod(piece * W_PIECE_COLS, I_DIM)
            copy(
                out=got("w_grouped", q)[:, piece * W_PIECE_COLS : (piece + 1) * W_PIECE_COLS, :]
                .rearrange("p (m i) t -> p m t i", i=RUN),
                in_=got("w_raw%d" % q, q)[:, c, :, part : part + W_PIECE_COLS].rearrange("p t (m i) -> p m t i", i=RUN),
            )

        def gpsimd_copy(out, in_):
            nc.gpsimd.tensor_scalar(out=out, in0=in_, scalar1=1.0, scalar2=0.0, op0=MULT, op1=ADD)

        def quantise_weight(q):
            passes = slice(q * HALVES, (q + 1) * HALVES)
            nc.vector.quantize_mx(
                out=w_codes[:, passes, :].rearrange("p c n -> p (c n)").bitcast(E4M3_X4),
                scales=w_scales[:, passes, :].rearrange("p c n -> p (c n)"),
                in_=got("w_grouped", q)[:].rearrange("p n t -> p (n t)"),
            )

        passes_done = {}
        passes_due = []
        to_store = []

        def multiply(n, q):
            b_tile, half = divmod(n, HALVES)
            if b_tile not in passes_done:
                new(psum, "acc", b_tile, F32, (P, I_DIM), bufs=2)
                passes_done[b_tile] = 0
            passes_done[b_tile] += 1
            words = slice(SLOT[q] * P, (SLOT[q] + 1) * P)
            nc.tensor.matmul_mx(
                out=got("acc", b_tile)[:],
                lhsT=got("d_codes", n)[:, words].bitcast(E5M2_X4),
                lhsT_scale=got("d_scales", n)[:, words],
                rhs=w_codes[:, q * HALVES + half, :].bitcast(E4M3_X4),
                rhs_scale=w_scales[:, q * HALVES + half, :],
                start=(passes_done[b_tile] == 1),
                stop=(passes_done[b_tile] == GATES * HALVES),
            )
            if passes_done[b_tile] == GATES * HALVES:
                to_store.extend([b_tile])

        def multiply_due():
            for i in range(min(PASSES_AT_ONCE, len(passes_due))):
                multiply(*passes_due[0])
                passes_due.remove(passes_due[0])

        def store_finished():
            for b_tile in to_store:
                result = work.tile([P, I_DIM], F32)
                halves = 2 if b_tile == B // P - 1 else 1
                for i in range(halves):
                    cols = slice(i * I_DIM // halves, (i + 1) * I_DIM // halves)
                    nc.scalar.copy(out=result[:, cols], in_=got("acc", b_tile)[:, cols])
                    nc.sync.dma_start(out=out[b_tile * P : (b_tile + 1) * P, cols], in_=result[:, cols])
            to_store.clear()

        def run(step, n, count=GROUPS):
            if 0 <= n < count:
                step(n)

        due = {
            2: [(0, 0), (1, 0)],
            3: [(2, 0), (0, 1), (1, 1), (2, 1)],
            4: [(3, 0), (3, 1)] + [(n, 2) for n in range(4)],
            5: [(n, 3) for n in range(4)] + [(4, GATE_F), (4, GATE_O)],
            6: [(4, GATE_I), (4, GATE_G)] + [(5, q) for q in SLOT],
            7: [(6, q) for q in SLOT] + [(7, q) for q in SLOT],
        }
        last = GROUPS - 1
        vector_pieces = {0: [(0, 0)]}
        gpsimd_pieces = {0: [(0, 1)], 1: [(0, 3)], 2: [(1, 3)], 3: [(2, 3)], 4: [(3, 3)]}
        scalar_pieces = {
            0: [(0, 2)],
            1: [(1, 0), (1, 1), (1, 2)],
            2: [(2, 0), (2, 1), (2, 2)],
            3: [(3, 0), (3, 1), (3, 2)],
        }

        warm(new(psum, "head", 0, tag=bank_of["s"]), HEAD_WARM)
        for j in range(-3, GROUPS):
            run(load_group, j + 3)
            if j == -3:
                load_weight(0, 0)
            if j == -2:
                load_weight(0, 1)
            if 0 < j + 1 < GATES:
                for c in range(HALVES):
                    load_weight(j + 1, c)

            run(op_e, j)
            run(turn_sum("pf", "pf"), j)
            run(op_d_g, j - 1, last)
            run(turn_g2, j)
            if j < last:
                multiply_due()
            run(turn_sum("q", "q"), j)
            run(op_d_cy, j)
            run(turn_gib, j)

            run(op_m2, j + 1)
            run(op_m1, j + 1)
            run(turn_sum("s", "m2", "m1"), j + 1)
            multiply_due()
            run(quantise_dgates, j - 1, last)
            for q, piece in vector_pieces.get(j, ()):
                regroup_weight(nc.vector.tensor_copy, q, piece)
            run(quantise_weight, j - 2, GATES)
            passes_due.extend(due.get(j, ()))
            multiply_due()
            run(op_hn, j + 1)
            if short(j + 1):
                run(op_r, j + 1)
            run(op_pf, j + 1)
            run(op_q, j + 1)
            if short(j + 1):
                run(op_pi, j + 1)
            for q, piece in gpsimd_pieces.get(j, ()):
                regroup_weight(gpsimd_copy, q, piece)
            run(act_tc, j + 1)

            run(op_d_f, j)
            run(turn_sum("hn", "hn"), j + 1)
            run(op_i_d, j)
            run(turn_ib, j + 1)
            run(op_d_o, j)
            run(op_d_i, j)
            run(turn_gcy, j + 1)
            if j < last:
                multiply_due()
                if j == 5:
                    multiply_due()
            else:
                quantise_dgates(j, 0, 2)
                op_d_g(j)
                quantise_dgates(j, 2, 3)
                quantise_dgates(j, 3, 4)
                for n, q in passes_due:
                    multiply(n, q)

            run(act("ib", "zi", SIGMOID, -1.0), j + 2)
            run(act("g", "zg", TANH), j + 2)
            run(act("fb", "zf", SIGMOID, -1.0), j + 2)
            run(act("ob", "zo", SIGMOID, -1.0), j + 2)
            run(act("g2", "g", SQUARE), j + 2)
            if short(j + 2):
                run(act("i", "zi", SIGMOID), j + 2)
            for q, piece in scalar_pieces.get(j, ()):
                regroup_weight(nc.scalar.copy, q, piece)
            store_finished()
